import numpy as np
import ml_dtypes

BF16 = ml_dtypes.bfloat16


def bf(x):
    return np.asarray(x, np.float32).astype(BF16)


def f32(x):
    return np.asarray(x, np.float32)


def f64(x):
    return np.asarray(x).astype(np.float64)


def striped(idx):
    return np.tile(idx.reshape(-1, 16).T, (8, 1))


E, V, B, T, H, D, N = 512, 4096, 8, 256, 4, 128, 2048
LN_EPS = 1e-6
KERNEL_EPS = 1e-3
PE_BASE = 10000.0
V_GAIN = 3.0
O_GAIN = 3.0


def pos_emb():
    pos = np.arange(T, dtype=np.float32)[:, None]
    div = np.exp(np.arange(0, E, 2, dtype=np.float32) * np.float32(-np.log(PE_BASE) / E))
    ang = pos * div
    pe = np.zeros((T, E), np.float32)
    pe[:, 0::2] = np.sin(ang)
    pe[:, 1::2] = np.cos(ang)
    return np.ascontiguousarray(pe.T)


def layer_norm(x, scale, bias):
    mu = x.mean(axis=0, keepdims=True)
    var = np.square(x - mu).mean(axis=0, keepdims=True)
    return (x - mu) / np.sqrt(var + LN_EPS) * scale + bias


def setup_inputs():
    return {
        "table": f32(np.random.standard_normal((E, V))),
        "pe": f32(pos_emb()),
        "ln_scale": f32(1.0 + 0.1 * np.random.standard_normal((E, 1))),
        "ln_bias": f32(0.1 * np.random.standard_normal((E, 1))),
        "wq": bf(np.random.standard_normal((E, E)) / np.sqrt(E)),
        "wk": bf(np.random.standard_normal((E, E)) / np.sqrt(E)),
        "wv": bf(V_GAIN * np.random.standard_normal((E, E)) / np.sqrt(E)),
        "wo": bf(O_GAIN * np.random.standard_normal((E, E)) / np.sqrt(E)),
        "offs": striped(np.random.permutation(np.tile(np.arange(V), 2))[:N]),
    }


def reference(table, pe, ln_scale, ln_bias, wq, wk, wv, wo, offs):
    idx = offs[:16].T.reshape(-1)
    x0 = f64(table)[:, idx] + np.tile(f64(pe), (1, B))
    hn = layer_norm(x0, f64(ln_scale), f64(ln_bias))
    q = f64(wq).T @ hn
    k = f64(wk).T @ hn
    v = f64(wv).T @ hn
    pq = np.maximum(q, 0.0) + KERNEL_EPS
    pk = np.maximum(k, 0.0) + KERNEL_EPS
    att = np.zeros((E, N), np.float64)
    for s in range(B):
        cols = slice(s * T, (s + 1) * T)
        for n in range(H):
            rows = slice(n * D, (n + 1) * D)
            kv = pk[rows, cols] @ v[rows, cols].T
            z = pk[rows, cols].sum(axis=1, keepdims=True)
            num = kv.T @ pq[rows, cols]
            den = (pq[rows, cols] * z).sum(axis=0, keepdims=True)
            att[rows, cols] = num / den
    return x0 + f64(wo).T @ att

@@ -1,0 +1,173 @@
+from contextlib import ExitStack
+
+import concourse.mybir as mybir
+from concourse.masks import make_identity
+
+F32, BF16, U16 = mybir.dt.float32, mybir.dt.bfloat16, mybir.dt.uint16
+ALU = mybir.AluOpType
+ACT = mybir.ActivationFunctionType
+
+P = 128
+E, V, N = 512, 4096, 2048
+T, H, D = 256, 4, 128
+CB = E // P
+CHUNK = 2 * T
+NCHUNK = N // CHUNK
+JB = CHUNK // P
+LN_EPS = 1e-6
+KERNEL_EPS = 1e-3
+VPAD = D + 16
+
+FLOPS = 4 * 2 * E * E * N + (N // T) * H * (2 * 2 * D * D * T + 2 * 2 * D * T)
+
+
+def tile_performerencoder_b_kernel(tc, table, pe, ln_scale, ln_bias, wq, wk, wv, wo, offs, out):
+    nc = tc.nc
+    with ExitStack() as ctx:
+        held = ctx.enter_context(tc.tile_pool(name="held", bufs=1))
+        work = ctx.enter_context(tc.tile_pool(name="work", bufs=2))
+        ahead = ctx.enter_context(tc.tile_pool(name="ahead", bufs=3))
+        psum = ctx.enter_context(tc.psum_pool(name="psum", bufs=8))
+
+        offsets = held.tile([P, N // 16], U16, name="offsets")
+        nc.sync.dma_start(offsets[:], offs)
+        pe_sb = held.tile([P, CB, T], F32, name="pe_sb")
+        table_sb = [held.tile([P, V], F32, name=f"table_sb{c}") for c in range(CB)]
+        for c in range(CB):
+            nc.sync.dma_start(pe_sb[:, c, :], pe[c * P : (c + 1) * P, :])
+            nc.sync.dma_start(table_sb[c][:], table[c * P : (c + 1) * P, :])
+        weights = {}
+        for name, w in (("wk", wk), ("wv", wv), ("wq", wq), ("wo", wo)):
+            weights[name] = held.tile([P, CB, E], BF16, name=name + "_sb")
+            nc.sync.dma_start(weights[name][:], w.rearrange("(b p) r -> p b r", p=P))
+
+        mean_f32 = held.tile([P, P], F32, name="mean_f32")
+        nc.vector.memset(mean_f32[:], 1.0 / E)
+        mean_bf = held.tile([P, P], BF16, name="mean_bf")
+        nc.vector.memset(mean_bf[:], 1.0 / E)
+        eps_col = held.tile([P, 1], F32, name="eps_col")
+        nc.vector.memset(eps_col[:], LN_EPS)
+        v_tiles = [held.tile([P, JB, H, VPAD], BF16, name=f"v_tile{i}") for i in range(2)]
+        for v_tile in v_tiles:
+            nc.gpsimd.memset(v_tile[:, :, :, D:VPAD], 1.0)
+
+        ln_rows = held.tile([CB, 2, P], F32, name="ln_rows")
+        nc.scalar.dma_start(ln_rows[:, 0, :], ln_scale.rearrange("(b p) o -> b (p o)", p=P))
+        nc.scalar.dma_start(ln_rows[:, 1, :], ln_bias.rearrange("(b p) o -> b (p o)", p=P))
+        ident = held.tile([CB, CB], F32, name="ident")
+        make_identity(nc, ident[:])
+        ln_ps = psum.tile([P, 2, CB], F32, tag="bank")
+        for i in range(2):
+            nc.tensor.matmul(ln_ps[:, i, :], lhsT=ln_rows[:, i, :], rhs=ident[:], start=True, stop=True)
+        ln_cols = held.tile([P, 2, CB], F32, name="ln_cols")
+        nc.vector.tensor_copy(ln_cols[:], ln_ps[:])
+
+        x0 = [held.tile([P, CB, CHUNK], F32, name=f"x0_{t}") for t in range(NCHUNK)]
+
+        def layer_norm(t):
+            mu_ps = psum.tile([P, CHUNK], F32, tag="bank")
+            for c in range(CB):
+                for s in range(CHUNK // T):
+                    first = (t * CHUNK + s * T) // 16
+                    nc.vector.tensor_tensor(
+                        x0[t][:, c, s * T : (s + 1) * T],
+                        table_sb[c][:].indirect(offsets[:, first : first + T // 16]),
+                        pe_sb[:, c, :],
+                        ALU.add,
+                    )
+                nc.tensor.matmul(mu_ps[:], lhsT=mean_f32[:], rhs=x0[t][:, c, :], start=(c == 0), stop=(c == CB - 1))
+            xc = work.tile([P, CB, CHUNK], F32)
+            sq = work.tile([P, CB, CHUNK], BF16)
+            var_ps = psum.tile([P, CHUNK], F32, tag="bank")
+            for c in range(CB):
+                nc.vector.tensor_tensor(xc[:, c, :], x0[t][:, c, :], mu_ps[:], ALU.subtract)
+                nc.scalar.activation(sq[:, c, :], xc[:, c, :], ACT.Square)
+                nc.tensor.matmul(var_ps[:], lhsT=mean_bf[:], rhs=sq[:, c, :], start=(c == 0), stop=(c == CB - 1))
+            rstd = work.tile([P, CHUNK], F32)
+            nc.scalar.activation(rstd[:], var_ps[:], ACT.Abs_reciprocal_sqrt, bias=eps_col[:])
+            hn = ahead.tile([P, CB, CHUNK], BF16)
+            for c in range(CB):
+                engine = nc.vector if c % 2 == 0 else nc.gpsimd
+                engine.tensor_tensor(xc[:, c, :], xc[:, c, :], rstd[:], ALU.mult)
+                nc.scalar.activation(
+                    hn[:, c, :], xc[:, c, :], ACT.Identity, bias=ln_cols[:, 1, c : c + 1], scale=ln_cols[:, 0, c : c + 1]
+                )
+            return hn
+
+        def project_kv(t, hn):
+            pk = work.tile([P, JB, E], BF16)
+            v_tile = v_tiles[t % 2]
+            for jb in range(JB):
+                k_ps = psum.tile([P, E], F32, tag="bank")
+                v_ps = psum.tile([P, E], F32, tag="bank")
+                for c in range(CB):
+                    entries = hn[:, c, jb * P : (jb + 1) * P]
+                    nc.tensor.matmul(k_ps[:], lhsT=entries, rhs=weights["wk"][:, c, :], start=(c == 0), stop=(c == CB - 1))
+                    nc.tensor.matmul(v_ps[:], lhsT=entries, rhs=weights["wv"][:, c, :], start=(c == 0), stop=(c == CB - 1))
+                nc.vector.tensor_scalar(pk[:, jb, :], k_ps[:], 0.0, KERNEL_EPS, ALU.max, ALU.add)
+                nc.scalar.activation(v_tile[:, jb, :, 0:D], v_ps[:].rearrange("p (n d) -> p n d", n=H), ACT.Copy)
+            return pk, v_tile
+
+        def products_kv(pk, v_tile):
+            kv_sb = work.tile([P, CHUNK // T, H, D], BF16)
+            z_sb = work.tile([P, CHUNK // T, H, D], BF16)
+            for s in range(CHUNK // T):
+                for n0 in range(0, H, 2):
+                    kv_ps = psum.tile([P, 2, T], F32, tag="bank")
+                    for i in range(2):
+                        n = n0 + i
+                        for half in range(T // P):
+                            jb = s * (T // P) + half
+                            nc.tensor.matmul(
+                                kv_ps[:, i, 0 : D + 1],
+                                lhsT=pk[:, jb, n * D : (n + 1) * D],
+                                rhs=v_tile[:, jb, n, 0 : D + 1],
+                                start=(half == 0),
+                                stop=(half == T // P - 1),
+                            )
+                    nc.scalar.activation(kv_sb[:, s, n0 : n0 + 2, :], kv_ps[:, :, 0:D], ACT.Copy)
+                    nc.scalar.activation(z_sb[:, s, n0 : n0 + 2, :], kv_ps[:, :, D : D + 1].to_broadcast([P, 2, D]), ACT.Copy)
+            return kv_sb, z_sb
+
+        def project_q(hn):
+            pq = work.tile([P, H, CHUNK], BF16)
+            for n in range(H):
+                q_ps = psum.tile([P, CHUNK], F32, tag="bank")
+                for c in range(CB):
+                    nc.tensor.matmul(q_ps[:], lhsT=weights["wq"][:, c, n * D : (n + 1) * D], rhs=hn[:, c, :], start=(c == 0), stop=(c == CB - 1))
+                nc.vector.tensor_scalar(pq[:, n, :], q_ps[:], 0.0, KERNEL_EPS, ALU.max, ALU.add)
+            return pq
+
+        def attend(pq, kv_sb, z_sb):
+            att = work.tile([P, H, CHUNK], BF16)
+            for n in range(H):
+                num_ps = psum.tile([P, CHUNK], F32, tag="bank")
+                den_ps = psum.tile([P, CHUNK], F32, tag="bank")
+                for s in range(CHUNK // T):
+                    cols = slice(s * T, (s + 1) * T)
+                    nc.tensor.matmul(num_ps[:, cols], lhsT=kv_sb[:, s, n, :], rhs=pq[:, n, cols], start=True, stop=True)
+                    nc.tensor.matmul(den_ps[:, cols], lhsT=z_sb[:, s, n, :], rhs=pq[:, n, cols], start=True, stop=True)
+                rsqrt_den = work.tile([P, CHUNK], F32)
+                nc.scalar.activation(rsqrt_den[:], den_ps[:], ACT.Abs_reciprocal_sqrt)
+                recip_den = work.tile([P, CHUNK], F32)
+                nc.scalar.activation(recip_den[:], rsqrt_den[:], ACT.Square)
+                nc.vector.tensor_tensor(att[:, n, :], num_ps[:], recip_den[:], ALU.mult)
+            return att
+
+        def project_out(t, att):
+            for c in range(CB):
+                o_ps = psum.tile([P, CHUNK], F32, tag="bank")
+                for n in range(H):
+                    nc.tensor.matmul(o_ps[:], lhsT=weights["wo"][:, n, c * P : (c + 1) * P], rhs=att[:, n, :], start=(n == 0), stop=(n == H - 1))
+                nc.vector.tensor_tensor(x0[t][:, c, :], o_ps[:], x0[t][:, c, :], ALU.add)
+                nc.sync.dma_start(out[c * P : (c + 1) * P, t * CHUNK : (t + 1) * CHUNK], x0[t][:, c, :])
+
+        hn = {0: layer_norm(0), 1: layer_norm(1)}
+        for t in range(NCHUNK):
+            pk, v_tile = project_kv(t, hn[t])
+            kv_sb, z_sb = products_kv(pk, v_tile)
+            pq = project_q(hn[t])
+            if t + 2 < NCHUNK:
+                hn[t + 2] = layer_norm(t + 2)
+            att = attend(pq, kv_sb, z_sb)
+            project_out(t, att)

@@ -11,12 +11,15 @@ P = 128
 E, V, N = 512, 4096, 2048
 T, H, D = 256, 4, 128
 CB = E // P
-CHUNK = 2 * T
-NCHUNK = N // CHUNK
-JB = CHUNK // P
 LN_EPS = 1e-6
 KERNEL_EPS = 1e-3
 VPAD = D + 16
+
+SEQS = (1, 2, 2, 2, 1)
+NCHUNK = len(SEQS)
+WIDTH = [T * n for n in SEQS]
+START = [T * sum(SEQS[:t]) for t in range(NCHUNK)]
+assert sum(WIDTH) == N
 
 FLOPS = 4 * 2 * E * E * N + (N // T) * H * (2 * 2 * D * D * T + 2 * 2 * D * T)
 
@@ -26,20 +29,24 @@ def tile_performerencoder_b_kernel(tc, table, pe, ln_scale, ln_bias, wq, wk, wv,
     with ExitStack() as ctx:
         held = ctx.enter_context(tc.tile_pool(name="held", bufs=1))
         work = ctx.enter_context(tc.tile_pool(name="work", bufs=2))
-        ahead = ctx.enter_context(tc.tile_pool(name="ahead", bufs=3))
         psum = ctx.enter_context(tc.psum_pool(name="psum", bufs=8))
 
         offsets = held.tile([P, N // 16], U16, name="offsets")
         nc.sync.dma_start(offsets[:], offs)
+        ln_rows = held.tile([CB, 2, P], F32, name="ln_rows")
+        nc.scalar.dma_start(ln_rows[:, 0, :], ln_scale.rearrange("(b p) o -> b (p o)", p=P))
+        nc.scalar.dma_start(ln_rows[:, 1, :], ln_bias.rearrange("(b p) o -> b (p o)", p=P))
         pe_sb = held.tile([P, CB, T], F32, name="pe_sb")
         table_sb = [held.tile([P, V], F32, name=f"table_sb{c}") for c in range(CB)]
         for c in range(CB):
-            nc.sync.dma_start(pe_sb[:, c, :], pe[c * P : (c + 1) * P, :])
-            nc.sync.dma_start(table_sb[c][:], table[c * P : (c + 1) * P, :])
+            rows = slice(c * P, (c + 1) * P)
+            nc.sync.dma_start(pe_sb[:, c, :], pe[rows, :])
+            nc.sync.dma_start(table_sb[c][:, 0 : V // 2], table[rows, 0 : V // 2])
+            nc.scalar.dma_start(table_sb[c][:, V // 2 : V], table[rows, V // 2 : V])
         weights = {}
-        for name, w in (("wk", wk), ("wv", wv), ("wq", wq), ("wo", wo)):
+        for name, w, queue in (("wk", wk, nc.sync), ("wv", wv, nc.scalar), ("wq", wq, nc.sync), ("wo", wo, nc.scalar)):
             weights[name] = held.tile([P, CB, E], BF16, name=name + "_sb")
-            nc.sync.dma_start(weights[name][:], w.rearrange("(b p) r -> p b r", p=P))
+            queue.dma_start(weights[name][:], w.rearrange("(b p) r -> p b r", p=P))
 
         mean_f32 = held.tile([P, P], F32, name="mean_f32")
         nc.vector.memset(mean_f32[:], 1.0 / E)
@@ -47,13 +54,10 @@ def tile_performerencoder_b_kernel(tc, table, pe, ln_scale, ln_bias, wq, wk, wv,
         nc.vector.memset(mean_bf[:], 1.0 / E)
         eps_col = held.tile([P, 1], F32, name="eps_col")
         nc.vector.memset(eps_col[:], LN_EPS)
-        v_tiles = [held.tile([P, JB, H, VPAD], BF16, name=f"v_tile{i}") for i in range(2)]
+        v_tiles = [held.tile([P, 2 * T // P, H, VPAD], BF16, name=f"v_tile{i}") for i in range(2)]
         for v_tile in v_tiles:
             nc.gpsimd.memset(v_tile[:, :, :, D:VPAD], 1.0)
 
-        ln_rows = held.tile([CB, 2, P], F32, name="ln_rows")
-        nc.scalar.dma_start(ln_rows[:, 0, :], ln_scale.rearrange("(b p) o -> b (p o)", p=P))
-        nc.scalar.dma_start(ln_rows[:, 1, :], ln_bias.rearrange("(b p) o -> b (p o)", p=P))
         ident = held.tile([CB, CB], F32, name="ident")
         make_identity(nc, ident[:])
         ln_ps = psum.tile([P, 2, CB], F32, tag="bank")
@@ -62,56 +66,64 @@ def tile_performerencoder_b_kernel(tc, table, pe, ln_scale, ln_bias, wq, wk, wv,
         ln_cols = held.tile([P, 2, CB], F32, name="ln_cols")
         nc.vector.tensor_copy(ln_cols[:], ln_ps[:])
 
-        x0 = [held.tile([P, CB, CHUNK], F32, name=f"x0_{t}") for t in range(NCHUNK)]
+        x0 = [held.tile([P, CB, WIDTH[t]], F32, name=f"x0_{t}") for t in range(NCHUNK)]
+        mu_ps, xc, sq, rstd, hn = {}, {}, {}, {}, {}
+        pk, pq, kv_sb, z_sb, att = {}, {}, {}, {}, {}
 
-        def layer_norm(t):
-            mu_ps = psum.tile([P, CHUNK], F32, tag="bank")
+        def look_up(t, c):
+            for s in range(SEQS[t]):
+                first = (START[t] + s * T) // 16
+                nc.vector.tensor_tensor(
+                    x0[t][:, c, s * T : (s + 1) * T],
+                    table_sb[c][:].indirect(offsets[:, first : first + T // 16]),
+                    pe_sb[:, c, :],
+                    ALU.add,
+                )
+
+        def add_to_mean(t, c):
+            if c == 0:
+                mu_ps[t] = psum.tile([P, WIDTH[t]], F32, name="mu_ps", tag="bank")
+            nc.tensor.matmul(mu_ps[t][:], lhsT=mean_f32[:], rhs=x0[t][:, c, :], start=(c == 0), stop=(c == CB - 1))
+
+        def centre_and_square(t):
+            xc[t] = work.tile([P, CB, WIDTH[t]], F32, name="xc", tag="xc")
+            sq[t] = work.tile([P, CB, WIDTH[t]], BF16, name="sq", tag="sq")
             for c in range(CB):
-                for s in range(CHUNK // T):
-                    first = (t * CHUNK + s * T) // 16
-                    nc.vector.tensor_tensor(
-                        x0[t][:, c, s * T : (s + 1) * T],
-                        table_sb[c][:].indirect(offsets[:, first : first + T // 16]),
-                        pe_sb[:, c, :],
-                        ALU.add,
-                    )
-                nc.tensor.matmul(mu_ps[:], lhsT=mean_f32[:], rhs=x0[t][:, c, :], start=(c == 0), stop=(c == CB - 1))
-            xc = work.tile([P, CB, CHUNK], F32)
-            sq = work.tile([P, CB, CHUNK], BF16)
-            var_ps = psum.tile([P, CHUNK], F32, tag="bank")
+                nc.vector.tensor_tensor(xc[t][:, c, :], x0[t][:, c, :], mu_ps[t][:], ALU.subtract)
+                nc.scalar.activation(sq[t][:, c, :], xc[t][:, c, :], ACT.Square)
+
+        def variance(t):
+            var_ps = psum.tile([P, WIDTH[t]], F32, tag="bank")
             for c in range(CB):
-                nc.vector.tensor_tensor(xc[:, c, :], x0[t][:, c, :], mu_ps[:], ALU.subtract)
-                nc.scalar.activation(sq[:, c, :], xc[:, c, :], ACT.Square)
-                nc.tensor.matmul(var_ps[:], lhsT=mean_bf[:], rhs=sq[:, c, :], start=(c == 0), stop=(c == CB - 1))
-            rstd = work.tile([P, CHUNK], F32)
-            nc.scalar.activation(rstd[:], var_ps[:], ACT.Abs_reciprocal_sqrt, bias=eps_col[:])
-            hn = ahead.tile([P, CB, CHUNK], BF16)
+                nc.tensor.matmul(var_ps[:], lhsT=mean_bf[:], rhs=sq[t][:, c, :], start=(c == 0), stop=(c == CB - 1))
+            rstd[t] = work.tile([P, WIDTH[t]], F32, name="rstd", tag="rstd")
+            nc.scalar.activation(rstd[t][:], var_ps[:], ACT.Abs_reciprocal_sqrt, bias=eps_col[:])
+
+        def normalise(t):
+            hn[t] = work.tile([P, CB, WIDTH[t]], BF16, name="hn", tag="hn")
             for c in range(CB):
                 engine = nc.vector if c % 2 == 0 else nc.gpsimd
-                engine.tensor_tensor(xc[:, c, :], xc[:, c, :], rstd[:], ALU.mult)
+                engine.tensor_tensor(xc[t][:, c, :], xc[t][:, c, :], rstd[t][:], ALU.mult)
                 nc.scalar.activation(
-                    hn[:, c, :], xc[:, c, :], ACT.Identity, bias=ln_cols[:, 1, c : c + 1], scale=ln_cols[:, 0, c : c + 1]
+                    hn[t][:, c, :], xc[t][:, c, :], ACT.Identity, bias=ln_cols[:, 1, c : c + 1], scale=ln_cols[:, 0, c : c + 1]
                 )
-            return hn
 
-        def project_kv(t, hn):
-            pk = work.tile([P, JB, E], BF16)
-            v_tile = v_tiles[t % 2]
-            for jb in range(JB):
-                k_ps = psum.tile([P, E], F32, tag="bank")
-                v_ps = psum.tile([P, E], F32, tag="bank")
-                for c in range(CB):
-                    entries = hn[:, c, jb * P : (jb + 1) * P]
-                    nc.tensor.matmul(k_ps[:], lhsT=entries, rhs=weights["wk"][:, c, :], start=(c == 0), stop=(c == CB - 1))
-                    nc.tensor.matmul(v_ps[:], lhsT=entries, rhs=weights["wv"][:, c, :], start=(c == 0), stop=(c == CB - 1))
-                nc.vector.tensor_scalar(pk[:, jb, :], k_ps[:], 0.0, KERNEL_EPS, ALU.max, ALU.add)
-                nc.scalar.activation(v_tile[:, jb, :, 0:D], v_ps[:].rearrange("p (n d) -> p n d", n=H), ACT.Copy)
-            return pk, v_tile
+        def project_kv(t, jb):
+            if jb == 0:
+                pk[t] = work.tile([P, WIDTH[t] // P, E], BF16, name="pk", tag="pk")
+            k_ps = psum.tile([P, E], F32, tag="bank")
+            v_ps = psum.tile([P, E], F32, tag="bank")
+            for c in range(CB):
+                entries = hn[t][:, c, jb * P : (jb + 1) * P]
+                nc.tensor.matmul(k_ps[:], lhsT=entries, rhs=weights["wk"][:, c, :], start=(c == 0), stop=(c == CB - 1))
+                nc.tensor.matmul(v_ps[:], lhsT=entries, rhs=weights["wv"][:, c, :], start=(c == 0), stop=(c == CB - 1))
+            nc.vector.tensor_scalar(pk[t][:, jb, :], k_ps[:], 0.0, KERNEL_EPS, ALU.max, ALU.add)
+            nc.scalar.activation(v_tiles[t % 2][:, jb, :, 0:D], v_ps[:].rearrange("p (n d) -> p n d", n=H), ACT.Copy)
 
-        def products_kv(pk, v_tile):
-            kv_sb = work.tile([P, CHUNK // T, H, D], BF16)
-            z_sb = work.tile([P, CHUNK // T, H, D], BF16)
-            for s in range(CHUNK // T):
+        def products_kv(t):
+            kv_sb[t] = work.tile([P, SEQS[t], H, D], BF16, name="kv_sb", tag="kv_sb")
+            z_sb[t] = work.tile([P, SEQS[t], H, D], BF16, name="z_sb", tag="z_sb")
+            for s in range(SEQS[t]):
                 for n0 in range(0, H, 2):
                     kv_ps = psum.tile([P, 2, T], F32, tag="bank")
                     for i in range(2):
@@ -120,54 +132,74 @@ def tile_performerencoder_b_kernel(tc, table, pe, ln_scale, ln_bias, wq, wk, wv,
                             jb = s * (T // P) + half
                             nc.tensor.matmul(
                                 kv_ps[:, i, 0 : D + 1],
-                                lhsT=pk[:, jb, n * D : (n + 1) * D],
-                                rhs=v_tile[:, jb, n, 0 : D + 1],
+                                lhsT=pk[t][:, jb, n * D : (n + 1) * D],
+                                rhs=v_tiles[t % 2][:, jb, n, 0 : D + 1],
                                 start=(half == 0),
                                 stop=(half == T // P - 1),
                             )
-                    nc.scalar.activation(kv_sb[:, s, n0 : n0 + 2, :], kv_ps[:, :, 0:D], ACT.Copy)
-                    nc.scalar.activation(z_sb[:, s, n0 : n0 + 2, :], kv_ps[:, :, D : D + 1].to_broadcast([P, 2, D]), ACT.Copy)
-            return kv_sb, z_sb
+                    nc.scalar.activation(kv_sb[t][:, s, n0 : n0 + 2, :], kv_ps[:, :, 0:D], ACT.Copy)
+                    nc.scalar.activation(z_sb[t][:, s, n0 : n0 + 2, :], kv_ps[:, :, D : D + 1].to_broadcast([P, 2, D]), ACT.Copy)
 
-        def project_q(hn):
-            pq = work.tile([P, H, CHUNK], BF16)
+        def project_q(t):
+            pq[t] = work.tile([P, H, WIDTH[t]], BF16, name="pq", tag="pq")
             for n in range(H):
-                q_ps = psum.tile([P, CHUNK], F32, tag="bank")
+                q_ps = psum.tile([P, WIDTH[t]], F32, tag="bank")
                 for c in range(CB):
-                    nc.tensor.matmul(q_ps[:], lhsT=weights["wq"][:, c, n * D : (n + 1) * D], rhs=hn[:, c, :], start=(c == 0), stop=(c == CB - 1))
-                nc.vector.tensor_scalar(pq[:, n, :], q_ps[:], 0.0, KERNEL_EPS, ALU.max, ALU.add)
-            return pq
+                    nc.tensor.matmul(q_ps[:], lhsT=weights["wq"][:, c, n * D : (n + 1) * D], rhs=hn[t][:, c, :], start=(c == 0), stop=(c == CB - 1))
+                nc.vector.tensor_scalar(pq[t][:, n, :], q_ps[:], 0.0, KERNEL_EPS, ALU.max, ALU.add)
 
-        def attend(pq, kv_sb, z_sb):
-            att = work.tile([P, H, CHUNK], BF16)
+        def attend(t, n):
+            if n == 0:
+                att[t] = work.tile([P, H, WIDTH[t]], BF16, name="att", tag="att")
+            num_ps = psum.tile([P, WIDTH[t]], F32, tag="bank")
+            den_ps = psum.tile([P, WIDTH[t]], F32, tag="bank")
+            for s in range(SEQS[t]):
+                cols = slice(s * T, (s + 1) * T)
+                nc.tensor.matmul(num_ps[:, cols], lhsT=kv_sb[t][:, s, n, :], rhs=pq[t][:, n, cols], start=True, stop=True)
+                nc.tensor.matmul(den_ps[:, cols], lhsT=z_sb[t][:, s, n, :], rhs=pq[t][:, n, cols], start=True, stop=True)
+            rsqrt_den = work.tile([P, WIDTH[t]], F32)
+            nc.scalar.activation(rsqrt_den[:], den_ps[:], ACT.Abs_reciprocal_sqrt)
+            recip_den = work.tile([P, WIDTH[t]], F32)
+            nc.scalar.activation(recip_den[:], rsqrt_den[:], ACT.Square)
+            nc.vector.tensor_tensor(att[t][:, n, :], num_ps[:], recip_den[:], ALU.mult)
+
+        def project_out(t, c):
+            o_ps = psum.tile([P, WIDTH[t]], F32, tag="bank")
             for n in range(H):
-                num_ps = psum.tile([P, CHUNK], F32, tag="bank")
-                den_ps = psum.tile([P, CHUNK], F32, tag="bank")
-                for s in range(CHUNK // T):
-                    cols = slice(s * T, (s + 1) * T)
-                    nc.tensor.matmul(num_ps[:, cols], lhsT=kv_sb[:, s, n, :], rhs=pq[:, n, cols], start=True, stop=True)
-                    nc.tensor.matmul(den_ps[:, cols], lhsT=z_sb[:, s, n, :], rhs=pq[:, n, cols], start=True, stop=True)
-                rsqrt_den = work.tile([P, CHUNK], F32)
-                nc.scalar.activation(rsqrt_den[:], den_ps[:], ACT.Abs_reciprocal_sqrt)
-                recip_den = work.tile([P, CHUNK], F32)
-                nc.scalar.activation(recip_den[:], rsqrt_den[:], ACT.Square)
-                nc.vector.tensor_tensor(att[:, n, :], num_ps[:], recip_den[:], ALU.mult)
-            return att
+                nc.tensor.matmul(o_ps[:], lhsT=weights["wo"][:, n, c * P : (c + 1) * P], rhs=att[t][:, n, :], start=(n == 0), stop=(n == H - 1))
+            nc.vector.tensor_tensor(x0[t][:, c, :], o_ps[:], x0[t][:, c, :], ALU.add)
+            nc.sync.dma_start(out[c * P : (c + 1) * P, START[t] : START[t] + WIDTH[t]], x0[t][:, c, :])
 
-        def project_out(t, att):
-            for c in range(CB):
-                o_ps = psum.tile([P, CHUNK], F32, tag="bank")
-                for n in range(H):
-                    nc.tensor.matmul(o_ps[:], lhsT=weights["wo"][:, n, c * P : (c + 1) * P], rhs=att[:, n, :], start=(n == 0), stop=(n == H - 1))
-                nc.vector.tensor_tensor(x0[t][:, c, :], o_ps[:], x0[t][:, c, :], ALU.add)
-                nc.sync.dma_start(out[c * P : (c + 1) * P, t * CHUNK : (t + 1) * CHUNK], x0[t][:, c, :])
+        for c in range(CB - 1):
+            for t in range(NCHUNK):
+                look_up(t, c)
+                add_to_mean(t, c)
+        look_up(0, CB - 1)
+        add_to_mean(0, CB - 1)
+        centre_and_square(0)
+        look_up(1, CB - 1)
+        variance(0)
+        add_to_mean(1, CB - 1)
+        normalise(0)
 
-        hn = {0: layer_norm(0), 1: layer_norm(1)}
         for t in range(NCHUNK):
-            pk, v_tile = project_kv(t, hn[t])
-            kv_sb, z_sb = products_kv(pk, v_tile)
-            pq = project_q(hn[t])
+            if t + 1 < NCHUNK:
+                centre_and_square(t + 1)
+            for jb in range(WIDTH[t] // P):
+                project_kv(t, jb)
+                if jb == 0 and t + 2 < NCHUNK:
+                    look_up(t + 2, CB - 1)
+            if t + 1 < NCHUNK:
+                variance(t + 1)
+            products_kv(t)
             if t + 2 < NCHUNK:
-                hn[t + 2] = layer_norm(t + 2)
-            att = attend(pq, kv_sb, z_sb)
-            project_out(t, att)
+                add_to_mean(t + 2, CB - 1)
+            if t + 1 < NCHUNK:
+                normalise(t + 1)
+            project_q(t)
+            for i in range(H):
+                attend(t, i)
+                if t > 0:
+                    project_out(t - 1, i)
+        for c in range(CB):
+            project_out(NCHUNK - 1, c)

@@ -15,7 +15,7 @@ LN_EPS = 1e-6
 KERNEL_EPS = 1e-3
 VPAD = D + 16
 
-SEQS = (1, 2, 2, 2, 1)
+SEQS = (2, 2, 2, 2)
 NCHUNK = len(SEQS)
 WIDTH = [T * n for n in SEQS]
 START = [T * sum(SEQS[:t]) for t in range(NCHUNK)]
@@ -41,12 +41,11 @@ def tile_performerencoder_b_kernel(tc, table, pe, ln_scale, ln_bias, wq, wk, wv,
         for c in range(CB):
             rows = slice(c * P, (c + 1) * P)
             nc.sync.dma_start(pe_sb[:, c, :], pe[rows, :])
-            nc.sync.dma_start(table_sb[c][:, 0 : V // 2], table[rows, 0 : V // 2])
-            nc.scalar.dma_start(table_sb[c][:, V // 2 : V], table[rows, V // 2 : V])
+            nc.sync.dma_start(table_sb[c][:], table[rows, :])
         weights = {}
-        for name, w, queue in (("wk", wk, nc.sync), ("wv", wv, nc.scalar), ("wq", wq, nc.sync), ("wo", wo, nc.scalar)):
+        for name, w in (("wk", wk), ("wv", wv), ("wq", wq), ("wo", wo)):
             weights[name] = held.tile([P, CB, E], BF16, name=name + "_sb")
-            queue.dma_start(weights[name][:], w.rearrange("(b p) r -> p b r", p=P))
+            nc.sync.dma_start(weights[name][:], w.rearrange("(b p) r -> p b r", p=P))
 
         mean_f32 = held.tile([P, P], F32, name="mean_f32")
         nc.vector.memset(mean_f32[:], 1.0 / E)
@@ -85,27 +84,32 @@ def tile_performerencoder_b_kernel(tc, table, pe, ln_scale, ln_bias, wq, wk, wv,
                 mu_ps[t] = psum.tile([P, WIDTH[t]], F32, name="mu_ps", tag="bank")
             nc.tensor.matmul(mu_ps[t][:], lhsT=mean_f32[:], rhs=x0[t][:, c, :], start=(c == 0), stop=(c == CB - 1))
 
-        def centre_and_square(t):
-            xc[t] = work.tile([P, CB, WIDTH[t]], F32, name="xc", tag="xc")
-            sq[t] = work.tile([P, CB, WIDTH[t]], BF16, name="sq", tag="sq")
+        def centre_and_square(t, s):
+            if s == 0:
+                xc[t] = work.tile([P, CB, WIDTH[t]], F32, name="xc", tag="xc")
+                sq[t] = work.tile([P, CB, WIDTH[t]], BF16, name="sq", tag="sq")
+            cols = slice(s * T, (s + 1) * T)
             for c in range(CB):
-                nc.vector.tensor_tensor(xc[t][:, c, :], x0[t][:, c, :], mu_ps[t][:], ALU.subtract)
-                nc.scalar.activation(sq[t][:, c, :], xc[t][:, c, :], ACT.Square)
+                nc.vector.tensor_tensor(xc[t][:, c, cols], x0[t][:, c, cols], mu_ps[t][:, cols], ALU.subtract)
+                nc.scalar.activation(sq[t][:, c, cols], xc[t][:, c, cols], ACT.Square)
 
-        def variance(t):
-            var_ps = psum.tile([P, WIDTH[t]], F32, tag="bank")
+        def variance(t, s):
+            cols = slice(s * T, (s + 1) * T)
+            var_ps = psum.tile([P, T], F32, tag="bank")
             for c in range(CB):
-                nc.tensor.matmul(var_ps[:], lhsT=mean_bf[:], rhs=sq[t][:, c, :], start=(c == 0), stop=(c == CB - 1))
-            rstd[t] = work.tile([P, WIDTH[t]], F32, name="rstd", tag="rstd")
-            nc.scalar.activation(rstd[t][:], var_ps[:], ACT.Abs_reciprocal_sqrt, bias=eps_col[:])
+                nc.tensor.matmul(var_ps[:], lhsT=mean_bf[:], rhs=sq[t][:, c, cols], start=(c == 0), stop=(c == CB - 1))
+            if s == 0:
+                rstd[t] = work.tile([P, WIDTH[t]], F32, name="rstd", tag="rstd")
+            nc.scalar.activation(rstd[t][:, cols], var_ps[:], ACT.Abs_reciprocal_sqrt, bias=eps_col[:])
 
-        def normalise(t):
-            hn[t] = work.tile([P, CB, WIDTH[t]], BF16, name="hn", tag="hn")
+        def normalise(t, s):
+            if s == 0:
+                hn[t] = work.tile([P, CB, WIDTH[t]], BF16, name="hn", tag="hn")
+            cols = slice(s * T, (s + 1) * T)
             for c in range(CB):
-                engine = nc.vector if c % 2 == 0 else nc.gpsimd
-                engine.tensor_tensor(xc[t][:, c, :], xc[t][:, c, :], rstd[t][:], ALU.mult)
+                nc.vector.tensor_tensor(xc[t][:, c, cols], xc[t][:, c, cols], rstd[t][:, cols], ALU.mult)
                 nc.scalar.activation(
-                    hn[t][:, c, :], xc[t][:, c, :], ACT.Identity, bias=ln_cols[:, 1, c : c + 1], scale=ln_cols[:, 0, c : c + 1]
+                    hn[t][:, c, cols], xc[t][:, c, cols], ACT.Identity, bias=ln_cols[:, 1, c : c + 1], scale=ln_cols[:, 0, c : c + 1]
                 )
 
         def project_kv(t, jb):
@@ -176,26 +180,32 @@ def tile_performerencoder_b_kernel(tc, table, pe, ln_scale, ln_bias, wq, wk, wv,
                 add_to_mean(t, c)
         look_up(0, CB - 1)
         add_to_mean(0, CB - 1)
-        centre_and_square(0)
         look_up(1, CB - 1)
-        variance(0)
         add_to_mean(1, CB - 1)
-        normalise(0)
+        for s in range(SEQS[0]):
+            centre_and_square(0, s)
+            variance(0, s)
+            normalise(0, s)
+        look_up(2, CB - 1)
+        add_to_mean(2, CB - 1)
 
         for t in range(NCHUNK):
             if t + 1 < NCHUNK:
-                centre_and_square(t + 1)
+                for s in range(SEQS[t + 1]):
+                    centre_and_square(t + 1, s)
             for jb in range(WIDTH[t] // P):
                 project_kv(t, jb)
-                if jb == 0 and t + 2 < NCHUNK:
-                    look_up(t + 2, CB - 1)
+                if jb == 0 and t + 3 < NCHUNK:
+                    look_up(t + 3, CB - 1)
             if t + 1 < NCHUNK:
-                variance(t + 1)
+                for s in range(SEQS[t + 1]):
+                    variance(t + 1, s)
             products_kv(t)
-            if t + 2 < NCHUNK:
-                add_to_mean(t + 2, CB - 1)
+            if t + 3 < NCHUNK:
+                add_to_mean(t + 3, CB - 1)
             if t + 1 < NCHUNK:
-                normalise(t + 1)
+                for s in range(SEQS[t + 1]):
+                    normalise(t + 1, s)
             project_q(t)
             for i in range(H):
                 attend(t, i)

@@ -53,6 +53,8 @@ def tile_performerencoder_b_kernel(tc, table, pe, ln_scale, ln_bias, wq, wk, wv,
         nc.vector.memset(mean_bf[:], 1.0 / E)
         eps_col = held.tile([P, 1], F32, name="eps_col")
         nc.vector.memset(eps_col[:], LN_EPS)
+        warm_up = held.tile([P, 1], F32, name="warm_up")
+        nc.scalar.activation(warm_up[:], eps_col[:], ACT.Abs_reciprocal_sqrt)
         v_tiles = [held.tile([P, 2 * T // P, H, VPAD], BF16, name=f"v_tile{i}") for i in range(2)]
         for v_tile in v_tiles:
             nc.gpsimd.memset(v_tile[:, :, :, D:VPAD], 1.0)

@@ -68,7 +68,7 @@ def tile_performerencoder_b_kernel(tc, table, pe, ln_scale, ln_bias, wq, wk, wv,
         nc.vector.tensor_copy(ln_cols[:], ln_ps[:])
 
         x0 = [held.tile([P, CB, WIDTH[t]], F32, name=f"x0_{t}") for t in range(NCHUNK)]
-        mu_ps, xc, sq, rstd, hn = {}, {}, {}, {}, {}
+        mu_ps, xc, sq, sq_sum, rstd, hn = {}, {}, {}, {}, {}, {}
         pk, pq, kv_sb, z_sb, att = {}, {}, {}, {}, {}
 
         def look_up(t, c):
@@ -89,17 +89,20 @@ def tile_performerencoder_b_kernel(tc, table, pe, ln_scale, ln_bias, wq, wk, wv,
         def centre_and_square(t, s):
             if s == 0:
                 xc[t] = work.tile([P, CB, WIDTH[t]], F32, name="xc", tag="xc")
-                sq[t] = work.tile([P, CB, WIDTH[t]], BF16, name="sq", tag="sq")
+                sq[t] = work.tile([P, CB, WIDTH[t]], F32, name="sq", tag="sq")
+                sq_sum[t] = work.tile([P, WIDTH[t]], BF16, name="sq_sum", tag="sq_sum")
             cols = slice(s * T, (s + 1) * T)
             for c in range(CB):
                 nc.vector.tensor_tensor(xc[t][:, c, cols], x0[t][:, c, cols], mu_ps[t][:, cols], ALU.subtract)
                 nc.scalar.activation(sq[t][:, c, cols], xc[t][:, c, cols], ACT.Square)
+                if c > 0:
+                    total = sq_sum[t][:, cols] if c == CB - 1 else sq[t][:, 0, cols]
+                    nc.vector.tensor_tensor(total, sq[t][:, 0, cols], sq[t][:, c, cols], ALU.add)
 
         def variance(t, s):
             cols = slice(s * T, (s + 1) * T)
             var_ps = psum.tile([P, T], F32, tag="bank")
-            for c in range(CB):
-                nc.tensor.matmul(var_ps[:], lhsT=mean_bf[:], rhs=sq[t][:, c, cols], start=(c == 0), stop=(c == CB - 1))
+            nc.tensor.matmul(var_ps[:], lhsT=mean_bf[:], rhs=sq_sum[t][:, cols], start=True, stop=True)
             if s == 0:
                 rstd[t] = work.tile([P, WIDTH[t]], F32, name="rstd", tag="rstd")
             nc.scalar.activation(rstd[t][:, cols], var_ps[:], ACT.Abs_reciprocal_sqrt, bias=eps_col[:])
@@ -182,33 +185,25 @@ def tile_performerencoder_b_kernel(tc, table, pe, ln_scale, ln_bias, wq, wk, wv,
                 add_to_mean(t, c)
         look_up(0, CB - 1)
         add_to_mean(0, CB - 1)
-        look_up(1, CB - 1)
-        add_to_mean(1, CB - 1)
         for s in range(SEQS[0]):
             centre_and_square(0, s)
             variance(0, s)
             normalise(0, s)
-        look_up(2, CB - 1)
-        add_to_mean(2, CB - 1)
 
         for t in range(NCHUNK):
-            if t + 1 < NCHUNK:
-                for s in range(SEQS[t + 1]):
-                    centre_and_square(t + 1, s)
             for jb in range(WIDTH[t] // P):
                 project_kv(t, jb)
-                if jb == 0 and t + 3 < NCHUNK:
-                    look_up(t + 3, CB - 1)
             if t + 1 < NCHUNK:
+                look_up(t + 1, CB - 1)
+                add_to_mean(t + 1, CB - 1)
                 for s in range(SEQS[t + 1]):
+                    centre_and_square(t + 1, s)
                     variance(t + 1, s)
             products_kv(t)
-            if t + 3 < NCHUNK:
-                add_to_mean(t + 3, CB - 1)
+            project_q(t)
             if t + 1 < NCHUNK:
                 for s in range(SEQS[t + 1]):
                     normalise(t + 1, s)
-            project_q(t)
             for i in range(H):
                 attend(t, i)
                 if t > 0:

@@ -68,7 +68,7 @@ def tile_performerencoder_b_kernel(tc, table, pe, ln_scale, ln_bias, wq, wk, wv,
         nc.vector.tensor_copy(ln_cols[:], ln_ps[:])
 
         x0 = [held.tile([P, CB, WIDTH[t]], F32, name=f"x0_{t}") for t in range(NCHUNK)]
-        mu_ps, xc, sq, sq_sum, rstd, hn = {}, {}, {}, {}, {}, {}
+        mu_ps, xc, sq, rstd, hn = {}, {}, {}, {}, {}
         pk, pq, kv_sb, z_sb, att = {}, {}, {}, {}, {}
 
         def look_up(t, c):
@@ -82,27 +82,30 @@ def tile_performerencoder_b_kernel(tc, table, pe, ln_scale, ln_bias, wq, wk, wv,
                 )
 
         def add_to_mean(t, c):
+            pieces = SEQS[t] if t == 0 else 1
+            width = WIDTH[t] // pieces
             if c == 0:
-                mu_ps[t] = psum.tile([P, WIDTH[t]], F32, name="mu_ps", tag="bank")
-            nc.tensor.matmul(mu_ps[t][:], lhsT=mean_f32[:], rhs=x0[t][:, c, :], start=(c == 0), stop=(c == CB - 1))
+                mu_ps[t] = [psum.tile([P, width], F32, name="mu_ps", tag="bank") for i in range(pieces)]
+            for i in range(pieces):
+                nc.tensor.matmul(
+                    mu_ps[t][i][:], lhsT=mean_f32[:], rhs=x0[t][:, c, i * width : (i + 1) * width], start=(c == 0), stop=(c == CB - 1)
+                )
 
         def centre_and_square(t, s):
             if s == 0:
                 xc[t] = work.tile([P, CB, WIDTH[t]], F32, name="xc", tag="xc")
-                sq[t] = work.tile([P, CB, WIDTH[t]], F32, name="sq", tag="sq")
-                sq_sum[t] = work.tile([P, WIDTH[t]], BF16, name="sq_sum", tag="sq_sum")
+                sq[t] = work.tile([P, CB, WIDTH[t]], BF16, name="sq", tag="sq")
             cols = slice(s * T, (s + 1) * T)
+            mean = mu_ps[t][s][:] if len(mu_ps[t]) > 1 else mu_ps[t][0][:, cols]
             for c in range(CB):
-                nc.vector.tensor_tensor(xc[t][:, c, cols], x0[t][:, c, cols], mu_ps[t][:, cols], ALU.subtract)
+                nc.vector.tensor_tensor(xc[t][:, c, cols], x0[t][:, c, cols], mean, ALU.subtract)
                 nc.scalar.activation(sq[t][:, c, cols], xc[t][:, c, cols], ACT.Square)
-                if c > 0:
-                    total = sq_sum[t][:, cols] if c == CB - 1 else sq[t][:, 0, cols]
-                    nc.vector.tensor_tensor(total, sq[t][:, 0, cols], sq[t][:, c, cols], ALU.add)
 
         def variance(t, s):
             cols = slice(s * T, (s + 1) * T)
             var_ps = psum.tile([P, T], F32, tag="bank")
-            nc.tensor.matmul(var_ps[:], lhsT=mean_bf[:], rhs=sq_sum[t][:, cols], start=True, stop=True)
+            for c in range(CB):
+                nc.tensor.matmul(var_ps[:], lhsT=mean_bf[:], rhs=sq[t][:, c, cols], start=(c == 0), stop=(c == CB - 1))
             if s == 0:
                 rstd[t] = work.tile([P, WIDTH[t]], F32, name="rstd", tag="rstd")
             nc.scalar.activation(rstd[t][:, cols], var_ps[:], ACT.Abs_reciprocal_sqrt, bias=eps_col[:])
@@ -185,25 +188,33 @@ def tile_performerencoder_b_kernel(tc, table, pe, ln_scale, ln_bias, wq, wk, wv,
                 add_to_mean(t, c)
         look_up(0, CB - 1)
         add_to_mean(0, CB - 1)
+        look_up(1, CB - 1)
+        add_to_mean(1, CB - 1)
         for s in range(SEQS[0]):
             centre_and_square(0, s)
             variance(0, s)
             normalise(0, s)
+        look_up(2, CB - 1)
+        add_to_mean(2, CB - 1)
 
         for t in range(NCHUNK):
-            for jb in range(WIDTH[t] // P):
-                project_kv(t, jb)
             if t + 1 < NCHUNK:
-                look_up(t + 1, CB - 1)
-                add_to_mean(t + 1, CB - 1)
                 for s in range(SEQS[t + 1]):
                     centre_and_square(t + 1, s)
+            for jb in range(WIDTH[t] // P):
+                project_kv(t, jb)
+                if jb == 0 and t + 3 < NCHUNK:
+                    look_up(t + 3, CB - 1)
+            if t + 1 < NCHUNK:
+                for s in range(SEQS[t + 1]):
                     variance(t + 1, s)
             products_kv(t)
-            project_q(t)
+            if t + 3 < NCHUNK:
+                add_to_mean(t + 3, CB - 1)
             if t + 1 < NCHUNK:
                 for s in range(SEQS[t + 1]):
                     normalise(t + 1, s)
+            project_q(t)
             for i in range(H):
                 attend(t, i)
                 if t > 0:

@@ -94,7 +94,10 @@ def tile_performerencoder_b_kernel(tc, table, pe, ln_scale, ln_bias, wq, wk, wv,
         def centre_and_square(t, s):
             if s == 0:
                 xc[t] = work.tile([P, CB, WIDTH[t]], F32, name="xc", tag="xc")
-                sq[t] = work.tile([P, CB, WIDTH[t]], BF16, name="sq", tag="sq")
+                if t == 0:
+                    sq[t] = work.tile([P, CB, WIDTH[t]], BF16, name="sq_first", tag="sq_first")
+                else:
+                    sq[t] = work.tile([P, CB, WIDTH[t]], F32, name="sq", tag="sq")
             cols = slice(s * T, (s + 1) * T)
             mean = mu_ps[t][s][:] if len(mu_ps[t]) > 1 else mu_ps[t][0][:, cols]
             for c in range(CB):
@@ -104,8 +107,15 @@ def tile_performerencoder_b_kernel(tc, table, pe, ln_scale, ln_bias, wq, wk, wv,
         def variance(t, s):
             cols = slice(s * T, (s + 1) * T)
             var_ps = psum.tile([P, T], F32, tag="bank")
-            for c in range(CB):
-                nc.tensor.matmul(var_ps[:], lhsT=mean_bf[:], rhs=sq[t][:, c, cols], start=(c == 0), stop=(c == CB - 1))
+            if t == 0:
+                for c in range(CB):
+                    nc.tensor.matmul(var_ps[:], lhsT=mean_bf[:], rhs=sq[t][:, c, cols], start=(c == 0), stop=(c == CB - 1))
+            else:
+                sq_pair = work.tile([P, 2, T], F32, name="sq_pair", tag="sq_pair")
+                nc.gpsimd.tensor_tensor(sq_pair[:], sq[t][:, 0:2, cols], sq[t][:, 2:4, cols], ALU.add)
+                sq_sum = work.tile([P, T], BF16, name="sq_sum", tag="sq_sum")
+                nc.gpsimd.tensor_tensor(sq_sum[:], sq_pair[:, 0, :], sq_pair[:, 1, :], ALU.add)
+                nc.tensor.matmul(var_ps[:], lhsT=mean_bf[:], rhs=sq_sum[:], start=True, stop=True)
             if s == 0:
                 rstd[t] = work.tile([P, WIDTH[t]], F32, name="rstd", tag="rstd")
             nc.scalar.activation(rstd[t][:, cols], var_ps[:], ACT.Abs_reciprocal_sqrt, bias=eps_col[:])

@@ -14,6 +14,8 @@ CB = E // P
 LN_EPS = 1e-6
 KERNEL_EPS = 1e-3
 VPAD = D + 16
+QUAD = 32
+NQ = D // QUAD
 
 SEQS = (2, 2, 2, 2)
 NCHUNK = len(SEQS)
@@ -43,9 +45,12 @@ def tile_performerencoder_b_kernel(tc, table, pe, ln_scale, ln_bias, wq, wk, wv,
             nc.sync.dma_start(pe_sb[:, c, :], pe[rows, :])
             nc.sync.dma_start(table_sb[c][:], table[rows, :])
         weights = {}
-        for name, w in (("wk", wk), ("wv", wv), ("wq", wq), ("wo", wo)):
+        for name, w in (("wk", wk), ("wv", wv), ("wq", wq)):
             weights[name] = held.tile([P, CB, E], BF16, name=name + "_sb")
             nc.sync.dma_start(weights[name][:], w.rearrange("(b p) r -> p b r", p=P))
+        wo_sb = held.tile([P, NQ, E], BF16, name="wo_sb")
+        for n in range(H):
+            nc.sync.dma_start(wo_sb[n * QUAD : (n + 1) * QUAD, :, :], wo[n * D : (n + 1) * D, :].rearrange("(g i) c -> i g c", i=QUAD))
 
         mean_f32 = held.tile([P, P], F32, name="mean_f32")
         nc.vector.memset(mean_f32[:], 1.0 / E)
@@ -69,7 +74,7 @@ def tile_performerencoder_b_kernel(tc, table, pe, ln_scale, ln_bias, wq, wk, wv,
 
         x0 = [held.tile([P, CB, WIDTH[t]], F32, name=f"x0_{t}") for t in range(NCHUNK)]
         mu_ps, xc, sq, rstd, hn = {}, {}, {}, {}, {}
-        pk, pq, kv_sb, z_sb, att = {}, {}, {}, {}, {}
+        pk, pq, kv_sb, z_sb, recip_den, att = {}, {}, {}, {}, {}, {}
 
         def look_up(t, c):
             for s in range(SEQS[t]):
@@ -144,7 +149,7 @@ def tile_performerencoder_b_kernel(tc, table, pe, ln_scale, ln_bias, wq, wk, wv,
 
         def products_kv(t):
             kv_sb[t] = work.tile([P, SEQS[t], H, D], BF16, name="kv_sb", tag="kv_sb")
-            z_sb[t] = work.tile([P, SEQS[t], H, D], BF16, name="z_sb", tag="z_sb")
+            z_sb[t] = work.tile([P, SEQS[t], H, QUAD], BF16, name="z_sb", tag="z_sb")
             for s in range(SEQS[t]):
                 for n0 in range(0, H, 2):
                     kv_ps = psum.tile([P, 2, T], F32, tag="bank")
@@ -160,7 +165,7 @@ def tile_performerencoder_b_kernel(tc, table, pe, ln_scale, ln_bias, wq, wk, wv,
                                 stop=(half == T // P - 1),
                             )
                     nc.scalar.activation(kv_sb[t][:, s, n0 : n0 + 2, :], kv_ps[:, :, 0:D], ACT.Copy)
-                    nc.scalar.activation(z_sb[t][:, s, n0 : n0 + 2, :], kv_ps[:, :, D : D + 1].to_broadcast([P, 2, D]), ACT.Copy)
+                    nc.scalar.activation(z_sb[t][:, s, n0 : n0 + 2, :], kv_ps[:, :, D : D + 1].to_broadcast([P, 2, QUAD]), ACT.Copy)
 
         def project_q(t):
             pq[t] = work.tile([P, H, WIDTH[t]], BF16, name="pq", tag="pq")
@@ -170,25 +175,38 @@ def tile_performerencoder_b_kernel(tc, table, pe, ln_scale, ln_bias, wq, wk, wv,
                     nc.tensor.matmul(q_ps[:], lhsT=weights["wq"][:, c, n * D : (n + 1) * D], rhs=hn[t][:, c, :], start=(c == 0), stop=(c == CB - 1))
                 nc.vector.tensor_scalar(pq[t][:, n, :], q_ps[:], 0.0, KERNEL_EPS, ALU.max, ALU.add)
 
-        def attend(t, n):
-            if n == 0:
-                att[t] = work.tile([P, H, WIDTH[t]], BF16, name="att", tag="att")
-            num_ps = psum.tile([P, WIDTH[t]], F32, tag="bank")
+
+        def denominators(t):
             den_ps = psum.tile([P, WIDTH[t]], F32, tag="bank")
             for s in range(SEQS[t]):
                 cols = slice(s * T, (s + 1) * T)
-                nc.tensor.matmul(num_ps[:, cols], lhsT=kv_sb[t][:, s, n, :], rhs=pq[t][:, n, cols], start=True, stop=True)
-                nc.tensor.matmul(den_ps[:, cols], lhsT=z_sb[t][:, s, n, :], rhs=pq[t][:, n, cols], start=True, stop=True)
+                for n in range(H):
+                    nc.tensor.matmul(den_ps[n * QUAD : (n + 1) * QUAD, cols], lhsT=z_sb[t][:, s, n, :], rhs=pq[t][:, n, cols], start=True, stop=True)
             rsqrt_den = work.tile([P, WIDTH[t]], F32)
             nc.scalar.activation(rsqrt_den[:], den_ps[:], ACT.Abs_reciprocal_sqrt)
-            recip_den = work.tile([P, WIDTH[t]], F32)
-            nc.scalar.activation(recip_den[:], rsqrt_den[:], ACT.Square)
-            nc.vector.tensor_tensor(att[t][:, n, :], num_ps[:], recip_den[:], ALU.mult)
+            recip_den[t] = work.tile([P, WIDTH[t]], F32, name="recip_den", tag="recip_den")
+            nc.scalar.activation(recip_den[t][:], rsqrt_den[:], ACT.Square)
+
+        def attend(t, g):
+            if g == 0:
+                att[t] = work.tile([P, NQ, WIDTH[t]], BF16, name="att", tag="att")
+            num_ps = psum.tile([P, WIDTH[t]], F32, tag="bank")
+            for s in range(SEQS[t]):
+                cols = slice(s * T, (s + 1) * T)
+                for n in range(H):
+                    nc.tensor.matmul(
+                        num_ps[n * QUAD : (n + 1) * QUAD, cols],
+                        lhsT=kv_sb[t][:, s, n, g * QUAD : (g + 1) * QUAD],
+                        rhs=pq[t][:, n, cols],
+                        start=True,
+                        stop=True,
+                    )
+            nc.vector.tensor_tensor(att[t][:, g, :], num_ps[:], recip_den[t][:], ALU.mult)
 
         def project_out(t, c):
             o_ps = psum.tile([P, WIDTH[t]], F32, tag="bank")
-            for n in range(H):
-                nc.tensor.matmul(o_ps[:], lhsT=weights["wo"][:, n, c * P : (c + 1) * P], rhs=att[t][:, n, :], start=(n == 0), stop=(n == H - 1))
+            for g in range(NQ):
+                nc.tensor.matmul(o_ps[:], lhsT=wo_sb[:, g, c * P : (c + 1) * P], rhs=att[t][:, g, :], start=(g == 0), stop=(g == NQ - 1))
             nc.vector.tensor_tensor(x0[t][:, c, :], o_ps[:], x0[t][:, c, :], ALU.add)
             nc.sync.dma_start(out[c * P : (c + 1) * P, START[t] : START[t] + WIDTH[t]], x0[t][:, c, :])
 
@@ -225,9 +243,13 @@ def tile_performerencoder_b_kernel(tc, table, pe, ln_scale, ln_bias, wq, wk, wv,
                 for s in range(SEQS[t + 1]):
                     normalise(t + 1, s)
             project_q(t)
-            for i in range(H):
-                attend(t, i)
-                if t > 0:
-                    project_out(t - 1, i)
+            if t > 0:
+                project_out(t - 1, 0)
+            denominators(t)
+            for g in range(NQ):
+                attend(t, g)
+            if t > 0:
+                for c in range(1, CB):
+                    project_out(t - 1, c)
         for c in range(CB):
             project_out(NCHUNK - 1, c)

@@ -203,12 +203,14 @@ def tile_performerencoder_b_kernel(tc, table, pe, ln_scale, ln_bias, wq, wk, wv,
                     )
             nc.vector.tensor_tensor(att[t][:, g, :], num_ps[:], recip_den[t][:], ALU.mult)
 
-        def project_out(t, c):
-            o_ps = psum.tile([P, WIDTH[t]], F32, tag="bank")
+        def project_out(t, c, first=0, width=None):
+            width = WIDTH[t] if width is None else width
+            cols = slice(first, first + width)
+            o_ps = psum.tile([P, width], F32, tag="bank")
             for g in range(NQ):
-                nc.tensor.matmul(o_ps[:], lhsT=wo_sb[:, g, c * P : (c + 1) * P], rhs=att[t][:, g, :], start=(g == 0), stop=(g == NQ - 1))
-            nc.vector.tensor_tensor(x0[t][:, c, :], o_ps[:], x0[t][:, c, :], ALU.add)
-            nc.sync.dma_start(out[c * P : (c + 1) * P, START[t] : START[t] + WIDTH[t]], x0[t][:, c, :])
+                nc.tensor.matmul(o_ps[:], lhsT=wo_sb[:, g, c * P : (c + 1) * P], rhs=att[t][:, g, cols], start=(g == 0), stop=(g == NQ - 1))
+            nc.vector.tensor_tensor(x0[t][:, c, cols], o_ps[:], x0[t][:, c, cols], ALU.add)
+            nc.sync.dma_start(out[c * P : (c + 1) * P, START[t] + first : START[t] + first + width], x0[t][:, c, cols])
 
         for c in range(CB - 1):
             for t in range(NCHUNK):
@@ -251,5 +253,7 @@ def tile_performerencoder_b_kernel(tc, table, pe, ln_scale, ln_bias, wq, wk, wv,
             if t > 0:
                 for c in range(1, CB):
                     project_out(t - 1, c)
-        for c in range(CB):
+        for c in range(CB - 1):
             project_out(NCHUNK - 1, c)
+        project_out(NCHUNK - 1, CB - 1, 0, WIDTH[NCHUNK - 1] - P)
+        project_out(NCHUNK - 1, CB - 1, WIDTH[NCHUNK - 1] - P, P)

@@ -91,6 +91,14 @@ def tile_performerencoder_b_kernel(tc, table, pe, ln_scale, ln_bias, wq, wk, wv,
             width = WIDTH[t] // pieces
             if c == 0:
                 mu_ps[t] = [psum.tile([P, width], F32, name="mu_ps", tag="bank") for i in range(pieces)]
+            if t == NCHUNK - 1 and c == CB - 1:
+                x_hi = held.tile([P, width], BF16, name="x_hi")
+                nc.scalar.activation(x_hi[:], x0[t][:, c, :], ACT.Copy)
+                x_lo = held.tile([P, width], BF16, name="x_lo")
+                nc.gpsimd.tensor_tensor(x_lo[:], x0[t][:, c, :], x_hi[:], ALU.subtract)
+                nc.tensor.matmul(mu_ps[t][0][:], lhsT=mean_bf[:], rhs=x_hi[:], start=False, stop=False)
+                nc.tensor.matmul(mu_ps[t][0][:], lhsT=mean_bf[:], rhs=x_lo[:], start=False, stop=True)
+                return
             for i in range(pieces):
                 nc.tensor.matmul(
                     mu_ps[t][i][:], lhsT=mean_f32[:], rhs=x0[t][:, c, i * width : (i + 1) * width], start=(c == 0), stop=(c == CB - 1)
@@ -147,33 +155,33 @@ def tile_performerencoder_b_kernel(tc, table, pe, ln_scale, ln_bias, wq, wk, wv,
             nc.vector.tensor_scalar(pk[t][:, jb, :], k_ps[:], 0.0, KERNEL_EPS, ALU.max, ALU.add)
             nc.scalar.activation(v_tiles[t % 2][:, jb, :, 0:D], v_ps[:].rearrange("p (n d) -> p n d", n=H), ACT.Copy)
 
-        def products_kv(t):
-            kv_sb[t] = work.tile([P, SEQS[t], H, D], BF16, name="kv_sb", tag="kv_sb")
-            z_sb[t] = work.tile([P, SEQS[t], H, QUAD], BF16, name="z_sb", tag="z_sb")
-            for s in range(SEQS[t]):
-                for n0 in range(0, H, 2):
-                    kv_ps = psum.tile([P, 2, T], F32, tag="bank")
-                    for i in range(2):
-                        n = n0 + i
-                        for half in range(T // P):
-                            jb = s * (T // P) + half
-                            nc.tensor.matmul(
-                                kv_ps[:, i, 0 : D + 1],
-                                lhsT=pk[t][:, jb, n * D : (n + 1) * D],
-                                rhs=v_tiles[t % 2][:, jb, n, 0 : D + 1],
-                                start=(half == 0),
-                                stop=(half == T // P - 1),
-                            )
-                    nc.scalar.activation(kv_sb[t][:, s, n0 : n0 + 2, :], kv_ps[:, :, 0:D], ACT.Copy)
-                    nc.scalar.activation(z_sb[t][:, s, n0 : n0 + 2, :], kv_ps[:, :, D : D + 1].to_broadcast([P, 2, QUAD]), ACT.Copy)
+        def products_kv(t, s):
+            if s == 0:
+                kv_sb[t] = work.tile([P, SEQS[t], H, D], BF16, name="kv_sb", tag="kv_sb")
+                z_sb[t] = work.tile([P, SEQS[t], H, QUAD], BF16, name="z_sb", tag="z_sb")
+            for n0 in range(0, H, 2):
+                kv_ps = psum.tile([P, 2, T], F32, tag="bank")
+                for i in range(2):
+                    n = n0 + i
+                    for half in range(T // P):
+                        jb = s * (T // P) + half
+                        nc.tensor.matmul(
+                            kv_ps[:, i, 0 : D + 1],
+                            lhsT=pk[t][:, jb, n * D : (n + 1) * D],
+                            rhs=v_tiles[t % 2][:, jb, n, 0 : D + 1],
+                            start=(half == 0),
+                            stop=(half == T // P - 1),
+                        )
+                nc.scalar.activation(kv_sb[t][:, s, n0 : n0 + 2, :], kv_ps[:, :, 0:D], ACT.Copy)
+                nc.scalar.activation(z_sb[t][:, s, n0 : n0 + 2, :], kv_ps[:, :, D : D + 1].to_broadcast([P, 2, QUAD]), ACT.Copy)
 
-        def project_q(t):
-            pq[t] = work.tile([P, H, WIDTH[t]], BF16, name="pq", tag="pq")
-            for n in range(H):
-                q_ps = psum.tile([P, WIDTH[t]], F32, tag="bank")
-                for c in range(CB):
-                    nc.tensor.matmul(q_ps[:], lhsT=weights["wq"][:, c, n * D : (n + 1) * D], rhs=hn[t][:, c, :], start=(c == 0), stop=(c == CB - 1))
-                nc.vector.tensor_scalar(pq[t][:, n, :], q_ps[:], 0.0, KERNEL_EPS, ALU.max, ALU.add)
+        def project_q(t, n):
+            if n == 0:
+                pq[t] = work.tile([P, H, WIDTH[t]], BF16, name="pq", tag="pq")
+            q_ps = psum.tile([P, WIDTH[t]], F32, tag="bank")
+            for c in range(CB):
+                nc.tensor.matmul(q_ps[:], lhsT=weights["wq"][:, c, n * D : (n + 1) * D], rhs=hn[t][:, c, :], start=(c == 0), stop=(c == CB - 1))
+            nc.vector.tensor_scalar(pq[t][:, n, :], q_ps[:], 0.0, KERNEL_EPS, ALU.max, ALU.add)
 
 
         def denominators(t):
@@ -238,22 +246,29 @@ def tile_performerencoder_b_kernel(tc, table, pe, ln_scale, ln_bias, wq, wk, wv,
             if t + 1 < NCHUNK:
                 for s in range(SEQS[t + 1]):
                     variance(t + 1, s)
-            products_kv(t)
-            if t + 3 < NCHUNK:
-                add_to_mean(t + 3, CB - 1)
+            for s in range(SEQS[t] - 1):
+                products_kv(t, s)
+            project_q(t, 0)
+            products_kv(t, SEQS[t] - 1)
             if t + 1 < NCHUNK:
                 for s in range(SEQS[t + 1]):
                     normalise(t + 1, s)
-            project_q(t)
+            for n in range(1, H):
+                project_q(t, n)
+            if t + 3 < NCHUNK:
+                add_to_mean(t + 3, CB - 1)
             if t > 0:
-                project_out(t - 1, 0)
+                for c in range(CB // 2):
+                    project_out(t - 1, c)
             denominators(t)
             for g in range(NQ):
                 attend(t, g)
             if t > 0:
-                for c in range(1, CB):
+                for c in range(CB // 2, CB):
                     project_out(t - 1, c)
         for c in range(CB - 1):
             project_out(NCHUNK - 1, c)
-        project_out(NCHUNK - 1, CB - 1, 0, WIDTH[NCHUNK - 1] - P)
-        project_out(NCHUNK - 1, CB - 1, WIDTH[NCHUNK - 1] - P, P)
+        half = WIDTH[NCHUNK - 1] // 2
+        project_out(NCHUNK - 1, CB - 1, 0, half)
+        project_out(NCHUNK - 1, CB - 1, half, half // 2)
+        project_out(NCHUNK - 1, CB - 1, half + half // 2, half // 2)

@@ -240,7 +240,8 @@ def tile_performerencoder_b_kernel(tc, table, pe, ln_scale, ln_bias, wq, wk, wv,
                 for s in range(SEQS[t + 1]):
                     centre_and_square(t + 1, s)
             for jb in range(WIDTH[t] // P):
-                project_kv(t, jb)
+                if (t, jb) != (1, 0):
+                    project_kv(t, jb)
                 if jb == 0 and t + 3 < NCHUNK:
                     look_up(t + 3, CB - 1)
             if t + 1 < NCHUNK:
@@ -260,6 +261,8 @@ def tile_performerencoder_b_kernel(tc, table, pe, ln_scale, ln_bias, wq, wk, wv,
             if t > 0:
                 for c in range(CB // 2):
                     project_out(t - 1, c)
+            else:
+                project_kv(1, 0)
             denominators(t)
             for g in range(NQ):
                 attend(t, g)

@@ -22,6 +22,7 @@ NCHUNK = len(SEQS)
 WIDTH = [T * n for n in SEQS]
 START = [T * sum(SEQS[:t]) for t in range(NCHUNK)]
 assert sum(WIDTH) == N
+PIECES = [[(0, T // 2), (T // 2, T // 2), (T, T)]] + [[(0, T), (T, T)] for t in range(1, NCHUNK)]
 
 FLOPS = 4 * 2 * E * E * N + (N // T) * H * (2 * 2 * D * D * T + 2 * 2 * D * T)
 
@@ -48,6 +49,8 @@ def tile_performerencoder_b_kernel(tc, table, pe, ln_scale, ln_bias, wq, wk, wv,
         for name, w in (("wk", wk), ("wv", wv), ("wq", wq)):
             weights[name] = held.tile([P, CB, E], BF16, name=name + "_sb")
             nc.sync.dma_start(weights[name][:], w.rearrange("(b p) r -> p b r", p=P))
+        pe_late = held.tile([P, T], F32, name="pe_late")
+        nc.sync.dma_start(pe_late[:], pe[(CB - 1) * P :, :])
         wo_sb = held.tile([P, NQ, E], BF16, name="wo_sb")
         for n in range(H):
             nc.sync.dma_start(wo_sb[n * QUAD : (n + 1) * QUAD, :, :], wo[n * D : (n + 1) * D, :].rearrange("(g i) c -> i g c", i=QUAD))
@@ -73,53 +76,61 @@ def tile_performerencoder_b_kernel(tc, table, pe, ln_scale, ln_bias, wq, wk, wv,
         nc.vector.tensor_copy(ln_cols[:], ln_ps[:])
 
         x0 = [held.tile([P, CB, WIDTH[t]], F32, name=f"x0_{t}") for t in range(NCHUNK)]
-        mu_ps, xc, sq, rstd, hn = {}, {}, {}, {}, {}
+        mu_ps, stand_in, xc, sq, rstd, hn = {}, {}, {}, {}, {}, {}
         pk, pq, kv_sb, z_sb, recip_den, att = {}, {}, {}, {}, {}, {}
 
         def look_up(t, c):
-            for s in range(SEQS[t]):
-                first = (START[t] + s * T) // 16
+            for first, width in PIECES[t if c == CB - 1 else 1]:
+                column = (START[t] + first) // 16
+                place = first % T
                 nc.vector.tensor_tensor(
-                    x0[t][:, c, s * T : (s + 1) * T],
-                    table_sb[c][:].indirect(offsets[:, first : first + T // 16]),
-                    pe_sb[:, c, :],
+                    x0[t][:, c, first : first + width],
+                    table_sb[c][:].indirect(offsets[:, column : column + width // 16]),
+                    pe_late[:] if t > 0 and c == CB - 1 else pe_sb[:, c, place : place + width],
                     ALU.add,
                 )
 
         def add_to_mean(t, c):
-            pieces = SEQS[t] if t == 0 else 1
-            width = WIDTH[t] // pieces
             if c == 0:
-                mu_ps[t] = [psum.tile([P, width], F32, name="mu_ps", tag="bank") for i in range(pieces)]
-            if t == NCHUNK - 1 and c == CB - 1:
-                x_hi = held.tile([P, width], BF16, name="x_hi")
-                nc.scalar.activation(x_hi[:], x0[t][:, c, :], ACT.Copy)
-                x_lo = held.tile([P, width], BF16, name="x_lo")
-                nc.gpsimd.tensor_tensor(x_lo[:], x0[t][:, c, :], x_hi[:], ALU.subtract)
-                nc.tensor.matmul(mu_ps[t][0][:], lhsT=mean_bf[:], rhs=x_hi[:], start=False, stop=False)
-                nc.tensor.matmul(mu_ps[t][0][:], lhsT=mean_bf[:], rhs=x_lo[:], start=False, stop=True)
+                mu_ps[t] = [psum.tile([P, width], F32, name="mu_ps", tag="bank") for first, width in (PIECES[0] if t == 0 else [(0, WIDTH[t])])]
+            if t > 0:
+                width = WIDTH[t]
+                if c < CB - 1:
+                    nc.tensor.matmul(mu_ps[t][0][:], lhsT=mean_f32[:], rhs=x0[t][:, c, :], start=(c == 0), stop=False)
+                if c == 0:
+                    stand_in[t] = held.tile([P, width], BF16, name=f"stand_in{t}")
+                    nc.scalar.activation(stand_in[t][:], x0[t][:, c, :], ACT.Copy)
+                    nc.tensor.matmul(mu_ps[t][0][:], lhsT=mean_bf[:], rhs=stand_in[t][:], start=False, stop=False)
+                if c == CB - 1:
+                    spread = work.tile([P, width], BF16, name="spread", tag="spread")
+                    nc.vector.tensor_tensor(spread[:], x0[t][:, c, :], stand_in[t][:], ALU.subtract)
+                    nc.tensor.matmul(mu_ps[t][0][:], lhsT=mean_bf[:], rhs=spread[:], start=False, stop=True)
                 return
-            for i in range(pieces):
+            for i, (first, width) in enumerate(PIECES[t]):
                 nc.tensor.matmul(
-                    mu_ps[t][i][:], lhsT=mean_f32[:], rhs=x0[t][:, c, i * width : (i + 1) * width], start=(c == 0), stop=(c == CB - 1)
+                    mu_ps[t][i][:], lhsT=mean_f32[:], rhs=x0[t][:, c, first : first + width], start=(c == 0), stop=(c == CB - 1)
                 )
 
-        def centre_and_square(t, s):
-            if s == 0:
+        def piece(t, i):
+            first, width = PIECES[t][i]
+            return slice(first, first + width)
+
+        def centre_and_square(t, i):
+            if i == 0:
                 xc[t] = work.tile([P, CB, WIDTH[t]], F32, name="xc", tag="xc")
                 if t == 0:
                     sq[t] = work.tile([P, CB, WIDTH[t]], BF16, name="sq_first", tag="sq_first")
                 else:
                     sq[t] = work.tile([P, CB, WIDTH[t]], F32, name="sq", tag="sq")
-            cols = slice(s * T, (s + 1) * T)
-            mean = mu_ps[t][s][:] if len(mu_ps[t]) > 1 else mu_ps[t][0][:, cols]
+            cols = piece(t, i)
+            mean = mu_ps[t][i][:] if t == 0 else mu_ps[t][0][:, cols]
             for c in range(CB):
                 nc.vector.tensor_tensor(xc[t][:, c, cols], x0[t][:, c, cols], mean, ALU.subtract)
                 nc.scalar.activation(sq[t][:, c, cols], xc[t][:, c, cols], ACT.Square)
 
-        def variance(t, s):
-            cols = slice(s * T, (s + 1) * T)
-            var_ps = psum.tile([P, T], F32, tag="bank")
+        def variance(t, i):
+            cols = piece(t, i)
+            var_ps = psum.tile([P, PIECES[t][i][1]], F32, tag="bank")
             if t == 0:
                 for c in range(CB):
                     nc.tensor.matmul(var_ps[:], lhsT=mean_bf[:], rhs=sq[t][:, c, cols], start=(c == 0), stop=(c == CB - 1))
@@ -129,14 +140,14 @@ def tile_performerencoder_b_kernel(tc, table, pe, ln_scale, ln_bias, wq, wk, wv,
                 sq_sum = work.tile([P, T], BF16, name="sq_sum", tag="sq_sum")
                 nc.gpsimd.tensor_tensor(sq_sum[:], sq_pair[:, 0, :], sq_pair[:, 1, :], ALU.add)
                 nc.tensor.matmul(var_ps[:], lhsT=mean_bf[:], rhs=sq_sum[:], start=True, stop=True)
-            if s == 0:
+            if i == 0:
                 rstd[t] = work.tile([P, WIDTH[t]], F32, name="rstd", tag="rstd")
             nc.scalar.activation(rstd[t][:, cols], var_ps[:], ACT.Abs_reciprocal_sqrt, bias=eps_col[:])
 
-        def normalise(t, s):
-            if s == 0:
+        def normalise(t, i):
+            if i == 0:
                 hn[t] = work.tile([P, CB, WIDTH[t]], BF16, name="hn", tag="hn")
-            cols = slice(s * T, (s + 1) * T)
+            cols = piece(t, i)
             for c in range(CB):
                 nc.vector.tensor_tensor(xc[t][:, c, cols], xc[t][:, c, cols], rstd[t][:, cols], ALU.mult)
                 nc.scalar.activation(
@@ -226,43 +237,48 @@ def tile_performerencoder_b_kernel(tc, table, pe, ln_scale, ln_bias, wq, wk, wv,
                 add_to_mean(t, c)
         look_up(0, CB - 1)
         add_to_mean(0, CB - 1)
+        for i in range(len(PIECES[0])):
+            centre_and_square(0, i)
+            variance(0, i)
+            normalise(0, i)
         look_up(1, CB - 1)
-        add_to_mean(1, CB - 1)
-        for s in range(SEQS[0]):
-            centre_and_square(0, s)
-            variance(0, s)
-            normalise(0, s)
-        look_up(2, CB - 1)
-        add_to_mean(2, CB - 1)
 
         for t in range(NCHUNK):
+            if t == 0:
+                project_kv(0, 0)
+                add_to_mean(1, CB - 1)
+            elif t > 1:
+                project_kv(t, 0)
+            project_kv(t, 1)
             if t + 1 < NCHUNK:
-                for s in range(SEQS[t + 1]):
-                    centre_and_square(t + 1, s)
-            for jb in range(WIDTH[t] // P):
-                if (t, jb) != (1, 0):
-                    project_kv(t, jb)
-                if jb == 0 and t + 3 < NCHUNK:
-                    look_up(t + 3, CB - 1)
-            if t + 1 < NCHUNK:
-                for s in range(SEQS[t + 1]):
-                    variance(t + 1, s)
-            for s in range(SEQS[t] - 1):
-                products_kv(t, s)
+                for i in range(len(PIECES[t + 1])):
+                    centre_and_square(t + 1, i)
+            for jb in range(2, WIDTH[t] // P):
+                project_kv(t, jb)
+            if t == 0:
+                look_up(2, CB - 1)
+            products_kv(t, 0)
             project_q(t, 0)
-            products_kv(t, SEQS[t] - 1)
             if t + 1 < NCHUNK:
-                for s in range(SEQS[t + 1]):
-                    normalise(t + 1, s)
-            for n in range(1, H):
-                project_q(t, n)
-            if t + 3 < NCHUNK:
-                add_to_mean(t + 3, CB - 1)
-            if t > 0:
+                variance(t + 1, 0)
+            products_kv(t, 1)
+            if t + 1 < NCHUNK:
+                normalise(t + 1, 0)
+            project_q(t, 1)
+            if t + 1 < NCHUNK:
+                variance(t + 1, 1)
+                normalise(t + 1, 1)
+            if t == 0:
+                add_to_mean(2, CB - 1)
+                look_up(3, CB - 1)
+            project_q(t, 2)
+            project_q(t, 3)
+            if t == 0:
+                add_to_mean(3, CB - 1)
+                project_kv(1, 0)
+            else:
                 for c in range(CB // 2):
                     project_out(t - 1, c)
-            else:
-                project_kv(1, 0)
             denominators(t)
             for g in range(NQ):
                 attend(t, g)

@@ -118,7 +118,7 @@ def tile_performerencoder_b_kernel(tc, table, pe, ln_scale, ln_bias, wq, wk, wv,
         def centre_and_square(t, i):
             if i == 0:
                 xc[t] = work.tile([P, CB, WIDTH[t]], F32, name="xc", tag="xc")
-                if t == 0:
+                if t <= 1:
                     sq[t] = work.tile([P, CB, WIDTH[t]], BF16, name="sq_first", tag="sq_first")
                 else:
                     sq[t] = work.tile([P, CB, WIDTH[t]], F32, name="sq", tag="sq")
@@ -131,7 +131,7 @@ def tile_performerencoder_b_kernel(tc, table, pe, ln_scale, ln_bias, wq, wk, wv,
         def variance(t, i):
             cols = piece(t, i)
             var_ps = psum.tile([P, PIECES[t][i][1]], F32, tag="bank")
-            if t == 0:
+            if t <= 1:
                 for c in range(CB):
                     nc.tensor.matmul(var_ps[:], lhsT=mean_bf[:], rhs=sq[t][:, c, cols], start=(c == 0), stop=(c == CB - 1))
             else:

@@ -24,6 +24,8 @@ START = [T * sum(SEQS[:t]) for t in range(NCHUNK)]
 assert sum(WIDTH) == N
 PIECES = [[(0, T // 2), (T // 2, T // 2), (T, T)]] + [[(0, T), (T, T)] for t in range(1, NCHUNK)]
 
+LATE_BLOCKS = [0, 1, 1, 2]
+
 FLOPS = 4 * 2 * E * E * N + (N // T) * H * (2 * 2 * D * D * T + 2 * 2 * D * T)
 
 
@@ -75,16 +77,23 @@ def tile_performerencoder_b_kernel(tc, table, pe, ln_scale, ln_bias, wq, wk, wv,
         ln_cols = held.tile([P, 2, CB], F32, name="ln_cols")
         nc.vector.tensor_copy(ln_cols[:], ln_ps[:])
 
-        x0 = [held.tile([P, CB, WIDTH[t]], F32, name=f"x0_{t}") for t in range(NCHUNK)]
+        x0 = [held.tile([P, CB - 1, WIDTH[t]], F32, name=f"x0_{t}") for t in range(NCHUNK)]
+        x_last = {}
+
+        def x(t, c, cols):
+            return x0[t][:, c, cols] if c < CB - 1 else x_last[t][:, cols]
+
         mu_ps, stand_in, xc, sq, rstd, hn = {}, {}, {}, {}, {}, {}
         pk, pq, kv_sb, z_sb, recip_den, att = {}, {}, {}, {}, {}, {}
 
         def look_up(t, c):
+            if c == CB - 1:
+                x_last[t] = work.tile([P, WIDTH[t]], F32, name="x_last", tag="x_last", bufs=3)
             for first, width in PIECES[t if c == CB - 1 else 1]:
                 column = (START[t] + first) // 16
                 place = first % T
                 nc.vector.tensor_tensor(
-                    x0[t][:, c, first : first + width],
+                    x(t, c, slice(first, first + width)),
                     table_sb[c][:].indirect(offsets[:, column : column + width // 16]),
                     pe_late[:] if t > 0 and c == CB - 1 else pe_sb[:, c, place : place + width],
                     ALU.add,
@@ -95,20 +104,27 @@ def tile_performerencoder_b_kernel(tc, table, pe, ln_scale, ln_bias, wq, wk, wv,
                 mu_ps[t] = [psum.tile([P, width], F32, name="mu_ps", tag="bank") for first, width in (PIECES[0] if t == 0 else [(0, WIDTH[t])])]
             if t > 0:
                 width = WIDTH[t]
-                if c < CB - 1:
+                late = LATE_BLOCKS[t]
+                if c < CB - late:
                     nc.tensor.matmul(mu_ps[t][0][:], lhsT=mean_f32[:], rhs=x0[t][:, c, :], start=(c == 0), stop=False)
                 if c == 0:
                     stand_in[t] = held.tile([P, width], BF16, name=f"stand_in{t}")
                     nc.scalar.activation(stand_in[t][:], x0[t][:, c, :], ACT.Copy)
-                    nc.tensor.matmul(mu_ps[t][0][:], lhsT=mean_bf[:], rhs=stand_in[t][:], start=False, stop=False)
+                    for i in range(late):
+                        nc.tensor.matmul(mu_ps[t][0][:], lhsT=mean_bf[:], rhs=stand_in[t][:], start=False, stop=False)
                 if c == CB - 1:
                     spread = work.tile([P, width], BF16, name="spread", tag="spread")
-                    nc.vector.tensor_tensor(spread[:], x0[t][:, c, :], stand_in[t][:], ALU.subtract)
+                    if late == 2:
+                        pair = work.tile([P, width], F32, name="pair", tag="pair", bufs=1)
+                        nc.vector.tensor_tensor(pair[:], x0[t][:, c - 1, :], x_last[t][:], ALU.add)
+                        nc.vector.scalar_tensor_tensor(spread[:], stand_in[t][:], -2.0, pair[:], ALU.mult, ALU.add)
+                    else:
+                        nc.vector.tensor_tensor(spread[:], x_last[t][:], stand_in[t][:], ALU.subtract)
                     nc.tensor.matmul(mu_ps[t][0][:], lhsT=mean_bf[:], rhs=spread[:], start=False, stop=True)
                 return
             for i, (first, width) in enumerate(PIECES[t]):
                 nc.tensor.matmul(
-                    mu_ps[t][i][:], lhsT=mean_f32[:], rhs=x0[t][:, c, first : first + width], start=(c == 0), stop=(c == CB - 1)
+                    mu_ps[t][i][:], lhsT=mean_f32[:], rhs=x(t, c, slice(first, first + width)), start=(c == 0), stop=(c == CB - 1)
                 )
 
         def piece(t, i):
@@ -125,7 +141,7 @@ def tile_performerencoder_b_kernel(tc, table, pe, ln_scale, ln_bias, wq, wk, wv,
             cols = piece(t, i)
             mean = mu_ps[t][i][:] if t == 0 else mu_ps[t][0][:, cols]
             for c in range(CB):
-                nc.vector.tensor_tensor(xc[t][:, c, cols], x0[t][:, c, cols], mean, ALU.subtract)
+                nc.vector.tensor_tensor(xc[t][:, c, cols], x(t, c, cols), mean, ALU.subtract)
                 nc.scalar.activation(sq[t][:, c, cols], xc[t][:, c, cols], ACT.Square)
 
         def variance(t, i):
@@ -228,8 +244,8 @@ def tile_performerencoder_b_kernel(tc, table, pe, ln_scale, ln_bias, wq, wk, wv,
             o_ps = psum.tile([P, width], F32, tag="bank")
             for g in range(NQ):
                 nc.tensor.matmul(o_ps[:], lhsT=wo_sb[:, g, c * P : (c + 1) * P], rhs=att[t][:, g, cols], start=(g == 0), stop=(g == NQ - 1))
-            nc.vector.tensor_tensor(x0[t][:, c, cols], o_ps[:], x0[t][:, c, cols], ALU.add)
-            nc.sync.dma_start(out[c * P : (c + 1) * P, START[t] + first : START[t] + first + width], x0[t][:, c, cols])
+            nc.vector.tensor_tensor(x(t, c, cols), o_ps[:], x(t, c, cols), ALU.add)
+            nc.sync.dma_start(out[c * P : (c + 1) * P, START[t] + first : START[t] + first + width], x(t, c, cols))
 
         for c in range(CB - 1):
             for t in range(NCHUNK):
@@ -244,47 +260,59 @@ def tile_performerencoder_b_kernel(tc, table, pe, ln_scale, ln_bias, wq, wk, wv,
         look_up(1, CB - 1)
 
         for t in range(NCHUNK):
+            early_norm = t + 1 < NCHUNK - 1
+            late_norm = t + 1 == NCHUNK - 1
+            if late_norm:
+                look_up(t + 1, CB - 1)
             if t == 0:
                 project_kv(0, 0)
                 add_to_mean(1, CB - 1)
             elif t > 1:
                 project_kv(t, 0)
             project_kv(t, 1)
-            if t + 1 < NCHUNK:
-                for i in range(len(PIECES[t + 1])):
-                    centre_and_square(t + 1, i)
-            for jb in range(2, WIDTH[t] // P):
-                project_kv(t, jb)
+            if early_norm:
+                centre_and_square(t + 1, 0)
+                centre_and_square(t + 1, 1)
+            project_kv(t, 2)
+            project_kv(t, 3)
+            if late_norm:
+                add_to_mean(t + 1, CB - 1)
+                centre_and_square(t + 1, 0)
+                centre_and_square(t + 1, 1)
             if t == 0:
                 look_up(2, CB - 1)
             products_kv(t, 0)
             project_q(t, 0)
-            if t + 1 < NCHUNK:
+            if early_norm:
                 variance(t + 1, 0)
             products_kv(t, 1)
-            if t + 1 < NCHUNK:
+            if early_norm:
                 normalise(t + 1, 0)
             project_q(t, 1)
-            if t + 1 < NCHUNK:
+            if early_norm:
                 variance(t + 1, 1)
                 normalise(t + 1, 1)
             if t == 0:
                 add_to_mean(2, CB - 1)
-                look_up(3, CB - 1)
             project_q(t, 2)
             project_q(t, 3)
+            if late_norm:
+                variance(t + 1, 0)
+                normalise(t + 1, 0)
+            if t > 0:
+                project_out(t - 1, 0)
+                project_out(t - 1, 1)
+            if late_norm:
+                variance(t + 1, 1)
+                normalise(t + 1, 1)
             if t == 0:
-                add_to_mean(3, CB - 1)
                 project_kv(1, 0)
-            else:
-                for c in range(CB // 2):
-                    project_out(t - 1, c)
             denominators(t)
             for g in range(NQ):
                 attend(t, g)
             if t > 0:
-                for c in range(CB // 2, CB):
-                    project_out(t - 1, c)
+                project_out(t - 1, 2)
+                project_out(t - 1, 3)
         for c in range(CB - 1):
             project_out(NCHUNK - 1, c)
         half = WIDTH[NCHUNK - 1] // 2

@@ -25,6 +25,7 @@ assert sum(WIDTH) == N
 PIECES = [[(0, T // 2), (T // 2, T // 2), (T, T)]] + [[(0, T), (T, T)] for t in range(1, NCHUNK)]
 
 LATE_BLOCKS = [0, 1, 1, 2]
+SUMMED_BY_TENSOR = [(0, 0), (0, 1), (0, 2), (1, 0)]
 
 FLOPS = 4 * 2 * E * E * N + (N // T) * H * (2 * 2 * D * D * T + 2 * 2 * D * T)
 
@@ -134,25 +135,25 @@ def tile_performerencoder_b_kernel(tc, table, pe, ln_scale, ln_bias, wq, wk, wv,
         def centre_and_square(t, i):
             if i == 0:
                 xc[t] = work.tile([P, CB, WIDTH[t]], F32, name="xc", tag="xc")
-                if t <= 1:
-                    sq[t] = work.tile([P, CB, WIDTH[t]], BF16, name="sq_first", tag="sq_first")
-                else:
-                    sq[t] = work.tile([P, CB, WIDTH[t]], F32, name="sq", tag="sq")
+            if (t, i) in SUMMED_BY_TENSOR:
+                sq[t, i] = work.tile([P, CB, PIECES[t][i][1]], BF16, name="sq_bf", tag="sq_bf", bufs=4)
+            else:
+                sq[t, i] = work.tile([P, CB, PIECES[t][i][1]], F32, name="sq", tag="sq", bufs=4)
             cols = piece(t, i)
             mean = mu_ps[t][i][:] if t == 0 else mu_ps[t][0][:, cols]
             for c in range(CB):
                 nc.vector.tensor_tensor(xc[t][:, c, cols], x(t, c, cols), mean, ALU.subtract)
-                nc.scalar.activation(sq[t][:, c, cols], xc[t][:, c, cols], ACT.Square)
+                nc.scalar.activation(sq[t, i][:, c, :], xc[t][:, c, cols], ACT.Square)
 
         def variance(t, i):
             cols = piece(t, i)
             var_ps = psum.tile([P, PIECES[t][i][1]], F32, tag="bank")
-            if t <= 1:
+            if (t, i) in SUMMED_BY_TENSOR:
                 for c in range(CB):
-                    nc.tensor.matmul(var_ps[:], lhsT=mean_bf[:], rhs=sq[t][:, c, cols], start=(c == 0), stop=(c == CB - 1))
+                    nc.tensor.matmul(var_ps[:], lhsT=mean_bf[:], rhs=sq[t, i][:, c, :], start=(c == 0), stop=(c == CB - 1))
             else:
                 sq_pair = work.tile([P, 2, T], F32, name="sq_pair", tag="sq_pair")
-                nc.gpsimd.tensor_tensor(sq_pair[:], sq[t][:, 0:2, cols], sq[t][:, 2:4, cols], ALU.add)
+                nc.gpsimd.tensor_tensor(sq_pair[:], sq[t, i][:, 0:2, :], sq[t, i][:, 2:4, :], ALU.add)
                 sq_sum = work.tile([P, T], BF16, name="sq_sum", tag="sq_sum")
                 nc.gpsimd.tensor_tensor(sq_sum[:], sq_pair[:, 0, :], sq_pair[:, 1, :], ALU.add)
                 nc.tensor.matmul(var_ps[:], lhsT=mean_bf[:], rhs=sq_sum[:], start=True, stop=True)

@@ -46,8 +46,11 @@ def tile_performerencoder_b_kernel(tc, table, pe, ln_scale, ln_bias, wq, wk, wv,
         table_sb = [held.tile([P, V], F32, name=f"table_sb{c}") for c in range(CB)]
         for c in range(CB):
             rows = slice(c * P, (c + 1) * P)
-            nc.sync.dma_start(pe_sb[:, c, :], pe[rows, :])
+            ahead = T if c < CB - 1 else PIECES[0][0][1]
+            nc.sync.dma_start(pe_sb[:, c, 0:ahead], pe[rows, 0:ahead])
             nc.sync.dma_start(table_sb[c][:], table[rows, :])
+            if ahead < T:
+                nc.sync.dma_start(pe_sb[:, c, ahead:], pe[rows, ahead:])
         weights = {}
         for name, w in (("wk", wk), ("wv", wv), ("wq", wq)):
             weights[name] = held.tile([P, CB, E], BF16, name=name + "_sb")
@@ -167,9 +170,12 @@ def tile_performerencoder_b_kernel(tc, table, pe, ln_scale, ln_bias, wq, wk, wv,
             cols = piece(t, i)
             for c in range(CB):
                 nc.vector.tensor_tensor(xc[t][:, c, cols], xc[t][:, c, cols], rstd[t][:, cols], ALU.mult)
-                nc.scalar.activation(
-                    hn[t][:, c, cols], xc[t][:, c, cols], ACT.Identity, bias=ln_cols[:, 1, c : c + 1], scale=ln_cols[:, 0, c : c + 1]
-                )
+                if (t, i, c) == (0, 0, 0):
+                    nc.vector.tensor_scalar(hn[t][:, c, cols], xc[t][:, c, cols], ln_cols[:, 0, c : c + 1], ln_cols[:, 1, c : c + 1], ALU.mult, ALU.add)
+                else:
+                    nc.scalar.activation(
+                        hn[t][:, c, cols], xc[t][:, c, cols], ACT.Identity, bias=ln_cols[:, 1, c : c + 1], scale=ln_cols[:, 0, c : c + 1]
+                    )
 
         def project_kv(t, jb):
             if jb == 0:
@@ -203,13 +209,15 @@ def tile_performerencoder_b_kernel(tc, table, pe, ln_scale, ln_bias, wq, wk, wv,
                 nc.scalar.activation(kv_sb[t][:, s, n0 : n0 + 2, :], kv_ps[:, :, 0:D], ACT.Copy)
                 nc.scalar.activation(z_sb[t][:, s, n0 : n0 + 2, :], kv_ps[:, :, D : D + 1].to_broadcast([P, 2, QUAD]), ACT.Copy)
 
-        def project_q(t, n):
-            if n == 0:
+        def project_q(t, n, first=0, width=None):
+            width = WIDTH[t] if width is None else width
+            cols = slice(first, first + width)
+            if t not in pq:
                 pq[t] = work.tile([P, H, WIDTH[t]], BF16, name="pq", tag="pq")
-            q_ps = psum.tile([P, WIDTH[t]], F32, tag="bank")
+            q_ps = psum.tile([P, width], F32, tag="bank")
             for c in range(CB):
-                nc.tensor.matmul(q_ps[:], lhsT=weights["wq"][:, c, n * D : (n + 1) * D], rhs=hn[t][:, c, :], start=(c == 0), stop=(c == CB - 1))
-            nc.vector.tensor_scalar(pq[t][:, n, :], q_ps[:], 0.0, KERNEL_EPS, ALU.max, ALU.add)
+                nc.tensor.matmul(q_ps[:], lhsT=weights["wq"][:, c, n * D : (n + 1) * D], rhs=hn[t][:, c, cols], start=(c == 0), stop=(c == CB - 1))
+            nc.vector.tensor_scalar(pq[t][:, n, cols], q_ps[:], 0.0, KERNEL_EPS, ALU.max, ALU.add)
 
 
         def denominators(t):
@@ -265,12 +273,12 @@ def tile_performerencoder_b_kernel(tc, table, pe, ln_scale, ln_bias, wq, wk, wv,
             late_norm = t + 1 == NCHUNK - 1
             if late_norm:
                 look_up(t + 1, CB - 1)
-            if t == 0:
-                project_kv(0, 0)
-                add_to_mean(1, CB - 1)
-            elif t > 1:
+            if t != 1:
                 project_kv(t, 0)
             project_kv(t, 1)
+            if t == 0:
+                add_to_mean(1, CB - 1)
+                project_q(0, 0, 0, T)
             if early_norm:
                 centre_and_square(t + 1, 0)
                 centre_and_square(t + 1, 1)
@@ -283,7 +291,10 @@ def tile_performerencoder_b_kernel(tc, table, pe, ln_scale, ln_bias, wq, wk, wv,
             if t == 0:
                 look_up(2, CB - 1)
             products_kv(t, 0)
-            project_q(t, 0)
+            if t == 0:
+                project_q(0, 0, T, T)
+            else:
+                project_q(t, 0)
             if early_norm:
                 variance(t + 1, 0)
             products_kv(t, 1)

@@ -65,6 +65,10 @@ def tile_performerencoder_b_kernel(tc, table, pe, ln_scale, ln_bias, wq, wk, wv,
         nc.vector.memset(mean_f32[:], 1.0 / E)
         mean_bf = held.tile([P, P], BF16, name="mean_bf")
         nc.vector.memset(mean_bf[:], 1.0 / E)
+        stand_in_weights = {}
+        for late in sorted(set(LATE_BLOCKS[1:])):
+            stand_in_weights[late] = held.tile([P, P], BF16, name=f"stand_in_weights{late}")
+            nc.vector.memset(stand_in_weights[late][:], late / E)
         eps_col = held.tile([P, 1], F32, name="eps_col")
         nc.vector.memset(eps_col[:], LN_EPS)
         warm_up = held.tile([P, 1], F32, name="warm_up")
@@ -114,8 +118,7 @@ def tile_performerencoder_b_kernel(tc, table, pe, ln_scale, ln_bias, wq, wk, wv,
                 if c == 0:
                     stand_in[t] = held.tile([P, width], BF16, name=f"stand_in{t}")
                     nc.scalar.activation(stand_in[t][:], x0[t][:, c, :], ACT.Copy)
-                    for i in range(late):
-                        nc.tensor.matmul(mu_ps[t][0][:], lhsT=mean_bf[:], rhs=stand_in[t][:], start=False, stop=False)
+                    nc.tensor.matmul(mu_ps[t][0][:], lhsT=stand_in_weights[late][:], rhs=stand_in[t][:], start=False, stop=False)
                 if c == CB - 1:
                     spread = work.tile([P, width], BF16, name="spread", tag="spread")
                     if late == 2:
@@ -156,7 +159,8 @@ def tile_performerencoder_b_kernel(tc, table, pe, ln_scale, ln_bias, wq, wk, wv,
                     nc.tensor.matmul(var_ps[:], lhsT=mean_bf[:], rhs=sq[t, i][:, c, :], start=(c == 0), stop=(c == CB - 1))
             else:
                 sq_pair = work.tile([P, 2, T], F32, name="sq_pair", tag="sq_pair")
-                nc.gpsimd.tensor_tensor(sq_pair[:], sq[t, i][:, 0:2, :], sq[t, i][:, 2:4, :], ALU.add)
+                for half in range(2):
+                    nc.gpsimd.tensor_tensor(sq_pair[:, half, :], sq[t, i][:, half, :], sq[t, i][:, half + 2, :], ALU.add)
                 sq_sum = work.tile([P, T], BF16, name="sq_sum", tag="sq_sum")
                 nc.gpsimd.tensor_tensor(sq_sum[:], sq_pair[:, 0, :], sq_pair[:, 1, :], ALU.add)
                 nc.tensor.matmul(var_ps[:], lhsT=mean_bf[:], rhs=sq_sum[:], start=True, stop=True)

@@ -42,7 +42,7 @@ def tile_performerencoder_b_kernel(tc, table, pe, ln_scale, ln_bias, wq, wk, wv,
         ln_rows = held.tile([CB, 2, P], F32, name="ln_rows")
         nc.scalar.dma_start(ln_rows[:, 0, :], ln_scale.rearrange("(b p) o -> b (p o)", p=P))
         nc.scalar.dma_start(ln_rows[:, 1, :], ln_bias.rearrange("(b p) o -> b (p o)", p=P))
-        pe_sb = held.tile([P, CB, T], F32, name="pe_sb")
+        pe_sb = held.tile([P, CB, 2 * T], F32, name="pe_sb")
         table_sb = [held.tile([P, V], F32, name=f"table_sb{c}") for c in range(CB)]
         for c in range(CB):
             rows = slice(c * P, (c + 1) * P)
@@ -50,7 +50,7 @@ def tile_performerencoder_b_kernel(tc, table, pe, ln_scale, ln_bias, wq, wk, wv,
             nc.sync.dma_start(pe_sb[:, c, 0:ahead], pe[rows, 0:ahead])
             nc.sync.dma_start(table_sb[c][:], table[rows, :])
             if ahead < T:
-                nc.sync.dma_start(pe_sb[:, c, ahead:], pe[rows, ahead:])
+                nc.sync.dma_start(pe_sb[:, c, ahead:T], pe[rows, ahead:])
         weights = {}
         for name, w in (("wk", wk), ("wv", wv), ("wq", wq)):
             weights[name] = held.tile([P, CB, E], BF16, name=name + "_sb")
@@ -97,7 +97,7 @@ def tile_performerencoder_b_kernel(tc, table, pe, ln_scale, ln_bias, wq, wk, wv,
         def look_up(t, c):
             if c == CB - 1:
                 x_last[t] = work.tile([P, WIDTH[t]], F32, name="x_last", tag="x_last", bufs=3)
-            for first, width in PIECES[t if c == CB - 1 else 1]:
+            for first, width in PIECES[t] if c == CB - 1 else [(0, WIDTH[t])]:
                 column = (START[t] + first) // 16
                 place = first % T
                 nc.vector.tensor_tensor(
@@ -106,6 +106,9 @@ def tile_performerencoder_b_kernel(tc, table, pe, ln_scale, ln_bias, wq, wk, wv,
                     pe_late[:] if t > 0 and c == CB - 1 else pe_sb[:, c, place : place + width],
                     ALU.add,
                 )
+
+        for c in range(CB - 1):
+            nc.scalar.activation(pe_sb[:, c, T : 2 * T], pe_sb[:, c, 0:T], ACT.Copy)
 
         def add_to_mean(t, c):
             if c == 0:

from contextlib import ExitStack

import concourse.mybir as mybir
from concourse.masks import make_identity

F32, BF16, U16 = mybir.dt.float32, mybir.dt.bfloat16, mybir.dt.uint16
ALU = mybir.AluOpType
ACT = mybir.ActivationFunctionType

P = 128
E, V, N = 512, 4096, 2048
T, H, D = 256, 4, 128
CB = E // P
LN_EPS = 1e-6
KERNEL_EPS = 1e-3
VPAD = D + 16
QUAD = 32
NQ = D // QUAD

SEQS = (2, 2, 2, 2)
NCHUNK = len(SEQS)
WIDTH = [T * n for n in SEQS]
START = [T * sum(SEQS[:t]) for t in range(NCHUNK)]
assert sum(WIDTH) == N
PIECES = [[(0, T // 2), (T // 2, T // 2), (T, T)]] + [[(0, T), (T, T)] for t in range(1, NCHUNK)]

LATE_BLOCKS = [0, 1, 1, 2]
SUMMED_BY_TENSOR = [(0, 0), (0, 1), (0, 2), (1, 0)]

FLOPS = 4 * 2 * E * E * N + (N // T) * H * (2 * 2 * D * D * T + 2 * 2 * D * T)


def tile_performerencoder_b_kernel(tc, table, pe, ln_scale, ln_bias, wq, wk, wv, wo, offs, out):
    nc = tc.nc
    with ExitStack() as ctx:
        held = ctx.enter_context(tc.tile_pool(name="held", bufs=1))
        work = ctx.enter_context(tc.tile_pool(name="work", bufs=2))
        psum = ctx.enter_context(tc.psum_pool(name="psum", bufs=8))

        offsets = held.tile([P, N // 16], U16, name="offsets")
        nc.sync.dma_start(offsets[:], offs)
        ln_rows = held.tile([CB, 2, P], F32, name="ln_rows")
        nc.scalar.dma_start(ln_rows[:, 0, :], ln_scale.rearrange("(b p) o -> b (p o)", p=P))
        nc.scalar.dma_start(ln_rows[:, 1, :], ln_bias.rearrange("(b p) o -> b (p o)", p=P))
        pe_sb = held.tile([P, CB, 2 * T], F32, name="pe_sb")
        table_sb = [held.tile([P, V], F32, name=f"table_sb{c}") for c in range(CB)]
        for c in range(CB):
            rows = slice(c * P, (c + 1) * P)
            ahead = T if c < CB - 1 else PIECES[0][0][1]
            nc.sync.dma_start(pe_sb[:, c, 0:ahead], pe[rows, 0:ahead])
            nc.sync.dma_start(table_sb[c][:], table[rows, :])
            if ahead < T:
                nc.sync.dma_start(pe_sb[:, c, ahead:T], pe[rows, ahead:])
        weights = {}
        for name, w in (("wk", wk), ("wv", wv), ("wq", wq)):
            weights[name] = held.tile([P, CB, E], BF16, name=name + "_sb")
            nc.sync.dma_start(weights[name][:], w.rearrange("(b p) r -> p b r", p=P))
        pe_late = held.tile([P, T], F32, name="pe_late")
        nc.sync.dma_start(pe_late[:], pe[(CB - 1) * P :, :])
        wo_sb = held.tile([P, NQ, E], BF16, name="wo_sb")
        for n in range(H):
            nc.sync.dma_start(wo_sb[n * QUAD : (n + 1) * QUAD, :, :], wo[n * D : (n + 1) * D, :].rearrange("(g i) c -> i g c", i=QUAD))

        mean_f32 = held.tile([P, P], F32, name="mean_f32")
        nc.vector.memset(mean_f32[:], 1.0 / E)
        mean_bf = held.tile([P, P], BF16, name="mean_bf")
        nc.vector.memset(mean_bf[:], 1.0 / E)
        stand_in_weights = {}
        for late in sorted(set(LATE_BLOCKS[1:])):
            stand_in_weights[late] = held.tile([P, P], BF16, name=f"stand_in_weights{late}")
            nc.vector.memset(stand_in_weights[late][:], late / E)
        eps_col = held.tile([P, 1], F32, name="eps_col")
        nc.vector.memset(eps_col[:], LN_EPS)
        warm_up = held.tile([P, 1], F32, name="warm_up")
        nc.scalar.activation(warm_up[:], eps_col[:], ACT.Abs_reciprocal_sqrt)
        v_tiles = [held.tile([P, 2 * T // P, H, VPAD], BF16, name=f"v_tile{i}") for i in range(2)]
        for v_tile in v_tiles:
            nc.gpsimd.memset(v_tile[:, :, :, D:VPAD], 1.0)

        ident = held.tile([CB, CB], F32, name="ident")
        make_identity(nc, ident[:])
        ln_ps = psum.tile([P, 2, CB], F32, tag="bank")
        for i in range(2):
            nc.tensor.matmul(ln_ps[:, i, :], lhsT=ln_rows[:, i, :], rhs=ident[:], start=True, stop=True)
        ln_cols = held.tile([P, 2, CB], F32, name="ln_cols")
        nc.vector.tensor_copy(ln_cols[:], ln_ps[:])

        x0 = [held.tile([P, CB - 1, WIDTH[t]], F32, name=f"x0_{t}") for t in range(NCHUNK)]
        x_last = {}

        def x(t, c, cols):
            return x0[t][:, c, cols] if c < CB - 1 else x_last[t][:, cols]

        mu_ps, stand_in, xc, sq, rstd, hn = {}, {}, {}, {}, {}, {}
        pk, pq, kv_sb, z_sb, recip_den, att = {}, {}, {}, {}, {}, {}

        def look_up(t, c):
            if c == CB - 1:
                x_last[t] = work.tile([P, WIDTH[t]], F32, name="x_last", tag="x_last", bufs=3)
            for first, width in PIECES[t] if c == CB - 1 else [(0, WIDTH[t])]:
                column = (START[t] + first) // 16
                place = first % T
                nc.vector.tensor_tensor(
                    x(t, c, slice(first, first + width)),
                    table_sb[c][:].indirect(offsets[:, column : column + width // 16]),
                    pe_late[:] if t > 0 and c == CB - 1 else pe_sb[:, c, place : place + width],
                    ALU.add,
                )

        for c in range(CB - 1):
            nc.scalar.activation(pe_sb[:, c, T : 2 * T], pe_sb[:, c, 0:T], ACT.Copy)

        def add_to_mean(t, c):
            if c == 0:
                mu_ps[t] = [psum.tile([P, width], F32, name="mu_ps", tag="bank") for first, width in (PIECES[0] if t == 0 else [(0, WIDTH[t])])]
            if t > 0:
                width = WIDTH[t]
                late = LATE_BLOCKS[t]
                if c < CB - late:
                    nc.tensor.matmul(mu_ps[t][0][:], lhsT=mean_f32[:], rhs=x0[t][:, c, :], start=(c == 0), stop=False)
                if c == 0:
                    stand_in[t] = held.tile([P, width], BF16, name=f"stand_in{t}")
                    nc.scalar.activation(stand_in[t][:], x0[t][:, c, :], ACT.Copy)
                    nc.tensor.matmul(mu_ps[t][0][:], lhsT=stand_in_weights[late][:], rhs=stand_in[t][:], start=False, stop=False)
                if c == CB - 1:
                    spread = work.tile([P, width], BF16, name="spread", tag="spread")
                    if late == 2:
                        pair = work.tile([P, width], F32, name="pair", tag="pair", bufs=1)
                        nc.vector.tensor_tensor(pair[:], x0[t][:, c - 1, :], x_last[t][:], ALU.add)
                        nc.vector.scalar_tensor_tensor(spread[:], stand_in[t][:], -2.0, pair[:], ALU.mult, ALU.add)
                    else:
                        nc.vector.tensor_tensor(spread[:], x_last[t][:], stand_in[t][:], ALU.subtract)
                    nc.tensor.matmul(mu_ps[t][0][:], lhsT=mean_bf[:], rhs=spread[:], start=False, stop=True)
                return
            for i, (first, width) in enumerate(PIECES[t]):
                nc.tensor.matmul(
                    mu_ps[t][i][:], lhsT=mean_f32[:], rhs=x(t, c, slice(first, first + width)), start=(c == 0), stop=(c == CB - 1)
                )

        def piece(t, i):
            first, width = PIECES[t][i]
            return slice(first, first + width)

        def centre_and_square(t, i):
            if i == 0:
                xc[t] = work.tile([P, CB, WIDTH[t]], F32, name="xc", tag="xc")
            if (t, i) in SUMMED_BY_TENSOR:
                sq[t, i] = work.tile([P, CB, PIECES[t][i][1]], BF16, name="sq_bf", tag="sq_bf", bufs=4)
            else:
                sq[t, i] = work.tile([P, CB, PIECES[t][i][1]], F32, name="sq", tag="sq", bufs=4)
            cols = piece(t, i)
            mean = mu_ps[t][i][:] if t == 0 else mu_ps[t][0][:, cols]
            for c in range(CB):
                nc.vector.tensor_tensor(xc[t][:, c, cols], x(t, c, cols), mean, ALU.subtract)
                nc.scalar.activation(sq[t, i][:, c, :], xc[t][:, c, cols], ACT.Square)

        def variance(t, i):
            cols = piece(t, i)
            var_ps = psum.tile([P, PIECES[t][i][1]], F32, tag="bank")
            if (t, i) in SUMMED_BY_TENSOR:
                for c in range(CB):
                    nc.tensor.matmul(var_ps[:], lhsT=mean_bf[:], rhs=sq[t, i][:, c, :], start=(c == 0), stop=(c == CB - 1))
            else:
                sq_pair = work.tile([P, 2, T], F32, name="sq_pair", tag="sq_pair")
                for half in range(2):
                    nc.gpsimd.tensor_tensor(sq_pair[:, half, :], sq[t, i][:, half, :], sq[t, i][:, half + 2, :], ALU.add)
                sq_sum = work.tile([P, T], BF16, name="sq_sum", tag="sq_sum")
                nc.gpsimd.tensor_tensor(sq_sum[:], sq_pair[:, 0, :], sq_pair[:, 1, :], ALU.add)
                nc.tensor.matmul(var_ps[:], lhsT=mean_bf[:], rhs=sq_sum[:], start=True, stop=True)
            if i == 0:
                rstd[t] = work.tile([P, WIDTH[t]], F32, name="rstd", tag="rstd")
            nc.scalar.activation(rstd[t][:, cols], var_ps[:], ACT.Abs_reciprocal_sqrt, bias=eps_col[:])

        def normalise(t, i):
            if i == 0:
                hn[t] = work.tile([P, CB, WIDTH[t]], BF16, name="hn", tag="hn")
            cols = piece(t, i)
            for c in range(CB):
                nc.vector.tensor_tensor(xc[t][:, c, cols], xc[t][:, c, cols], rstd[t][:, cols], ALU.mult)
                if (t, i, c) == (0, 0, 0):
                    nc.vector.tensor_scalar(hn[t][:, c, cols], xc[t][:, c, cols], ln_cols[:, 0, c : c + 1], ln_cols[:, 1, c : c + 1], ALU.mult, ALU.add)
                else:
                    nc.scalar.activation(
                        hn[t][:, c, cols], xc[t][:, c, cols], ACT.Identity, bias=ln_cols[:, 1, c : c + 1], scale=ln_cols[:, 0, c : c + 1]
                    )

        def project_kv(t, jb):
            if jb == 0:
                pk[t] = work.tile([P, WIDTH[t] // P, E], BF16, name="pk", tag="pk")
            k_ps = psum.tile([P, E], F32, tag="bank")
            v_ps = psum.tile([P, E], F32, tag="bank")
            for c in range(CB):
                entries = hn[t][:, c, jb * P : (jb + 1) * P]
                nc.tensor.matmul(k_ps[:], lhsT=entries, rhs=weights["wk"][:, c, :], start=(c == 0), stop=(c == CB - 1))
                nc.tensor.matmul(v_ps[:], lhsT=entries, rhs=weights["wv"][:, c, :], start=(c == 0), stop=(c == CB - 1))
            nc.vector.tensor_scalar(pk[t][:, jb, :], k_ps[:], 0.0, KERNEL_EPS, ALU.max, ALU.add)
            nc.scalar.activation(v_tiles[t % 2][:, jb, :, 0:D], v_ps[:].rearrange("p (n d) -> p n d", n=H), ACT.Copy)

        def products_kv(t, s):
            if s == 0:
                kv_sb[t] = work.tile([P, SEQS[t], H, D], BF16, name="kv_sb", tag="kv_sb")
                z_sb[t] = work.tile([P, SEQS[t], H, QUAD], BF16, name="z_sb", tag="z_sb")
            for n0 in range(0, H, 2):
                kv_ps = psum.tile([P, 2, T], F32, tag="bank")
                for i in range(2):
                    n = n0 + i
                    for half in range(T // P):
                        jb = s * (T // P) + half
                        nc.tensor.matmul(
                            kv_ps[:, i, 0 : D + 1],
                            lhsT=pk[t][:, jb, n * D : (n + 1) * D],
                            rhs=v_tiles[t % 2][:, jb, n, 0 : D + 1],
                            start=(half == 0),
                            stop=(half == T // P - 1),
                        )
                nc.scalar.activation(kv_sb[t][:, s, n0 : n0 + 2, :], kv_ps[:, :, 0:D], ACT.Copy)
                nc.scalar.activation(z_sb[t][:, s, n0 : n0 + 2, :], kv_ps[:, :, D : D + 1].to_broadcast([P, 2, QUAD]), ACT.Copy)

        def project_q(t, n, first=0, width=None):
            width = WIDTH[t] if width is None else width
            cols = slice(first, first + width)
            if t not in pq:
                pq[t] = work.tile([P, H, WIDTH[t]], BF16, name="pq", tag="pq")
            q_ps = psum.tile([P, width], F32, tag="bank")
            for c in range(CB):
                nc.tensor.matmul(q_ps[:], lhsT=weights["wq"][:, c, n * D : (n + 1) * D], rhs=hn[t][:, c, cols], start=(c == 0), stop=(c == CB - 1))
            nc.vector.tensor_scalar(pq[t][:, n, cols], q_ps[:], 0.0, KERNEL_EPS, ALU.max, ALU.add)


        def denominators(t):
            den_ps = psum.tile([P, WIDTH[t]], F32, tag="bank")
            for s in range(SEQS[t]):
                cols = slice(s * T, (s + 1) * T)
                for n in range(H):
                    nc.tensor.matmul(den_ps[n * QUAD : (n + 1) * QUAD, cols], lhsT=z_sb[t][:, s, n, :], rhs=pq[t][:, n, cols], start=True, stop=True)
            rsqrt_den = work.tile([P, WIDTH[t]], F32)
            nc.scalar.activation(rsqrt_den[:], den_ps[:], ACT.Abs_reciprocal_sqrt)
            recip_den[t] = work.tile([P, WIDTH[t]], F32, name="recip_den", tag="recip_den")
            nc.scalar.activation(recip_den[t][:], rsqrt_den[:], ACT.Square)

        def attend(t, g):
            if g == 0:
                att[t] = work.tile([P, NQ, WIDTH[t]], BF16, name="att", tag="att")
            num_ps = psum.tile([P, WIDTH[t]], F32, tag="bank")
            for s in range(SEQS[t]):
                cols = slice(s * T, (s + 1) * T)
                for n in range(H):
                    nc.tensor.matmul(
                        num_ps[n * QUAD : (n + 1) * QUAD, cols],
                        lhsT=kv_sb[t][:, s, n, g * QUAD : (g + 1) * QUAD],
                        rhs=pq[t][:, n, cols],
                        start=True,
                        stop=True,
                    )
            nc.vector.tensor_tensor(att[t][:, g, :], num_ps[:], recip_den[t][:], ALU.mult)

        def project_out(t, c, first=0, width=None):
            width = WIDTH[t] if width is None else width
            cols = slice(first, first + width)
            o_ps = psum.tile([P, width], F32, tag="bank")
            for g in range(NQ):
                nc.tensor.matmul(o_ps[:], lhsT=wo_sb[:, g, c * P : (c + 1) * P], rhs=att[t][:, g, cols], start=(g == 0), stop=(g == NQ - 1))
            nc.vector.tensor_tensor(x(t, c, cols), o_ps[:], x(t, c, cols), ALU.add)
            nc.sync.dma_start(out[c * P : (c + 1) * P, START[t] + first : START[t] + first + width], x(t, c, cols))

        for c in range(CB - 1):
            for t in range(NCHUNK):
                look_up(t, c)
                add_to_mean(t, c)
        look_up(0, CB - 1)
        add_to_mean(0, CB - 1)
        for i in range(len(PIECES[0])):
            centre_and_square(0, i)
            variance(0, i)
            normalise(0, i)
        look_up(1, CB - 1)

        for t in range(NCHUNK):
            early_norm = t + 1 < NCHUNK - 1
            late_norm = t + 1 == NCHUNK - 1
            if late_norm:
                look_up(t + 1, CB - 1)
            if t != 1:
                project_kv(t, 0)
            project_kv(t, 1)
            if t == 0:
                add_to_mean(1, CB - 1)
                project_q(0, 0, 0, T)
            if early_norm:
                centre_and_square(t + 1, 0)
                centre_and_square(t + 1, 1)
            project_kv(t, 2)
            project_kv(t, 3)
            if late_norm:
                add_to_mean(t + 1, CB - 1)
                centre_and_square(t + 1, 0)
                centre_and_square(t + 1, 1)
            if t == 0:
                look_up(2, CB - 1)
            products_kv(t, 0)
            if t == 0:
                project_q(0, 0, T, T)
            else:
                project_q(t, 0)
            if early_norm:
                variance(t + 1, 0)
            products_kv(t, 1)
            if early_norm:
                normalise(t + 1, 0)
            project_q(t, 1)
            if early_norm:
                variance(t + 1, 1)
                normalise(t + 1, 1)
            if t == 0:
                add_to_mean(2, CB - 1)
            project_q(t, 2)
            project_q(t, 3)
            if late_norm:
                variance(t + 1, 0)
                normalise(t + 1, 0)
            if t > 0:
                project_out(t - 1, 0)
                project_out(t - 1, 1)
            if late_norm:
                variance(t + 1, 1)
                normalise(t + 1, 1)
            if t == 0:
                project_kv(1, 0)
            denominators(t)
            for g in range(NQ):
                attend(t, g)
            if t > 0:
                project_out(t - 1, 2)
                project_out(t - 1, 3)
        for c in range(CB - 1):
            project_out(NCHUNK - 1, c)
        half = WIDTH[NCHUNK - 1] // 2
        project_out(NCHUNK - 1, CB - 1, 0, half)
        project_out(NCHUNK - 1, CB - 1, half, half // 2)
        project_out(NCHUNK - 1, CB - 1, half + half // 2, half // 2)
